import numpy as np
import ml_dtypes


def mxq(x, axis, fmt="e4m3"):
    dtype, down = {"e4m3": (ml_dtypes.float8_e4m3fn, 7), "e5m2": (ml_dtypes.float8_e5m2, 14)}[fmt]
    v = np.moveaxis(np.asarray(x, np.float32).astype(ml_dtypes.bfloat16).astype(np.float64), axis, -1)
    blocks = v.reshape(v.shape[:-1] + (-1, 32))
    amax = np.abs(blocks).max(-1, keepdims=True)
    byte = np.maximum(np.where(amax > 0, np.frexp(amax)[1] - 1 + 127, 0) - down, 1)
    scale = np.exp2(byte - 127.0)
    codes = (blocks / scale).astype(np.float32).astype(dtype).astype(np.float64)
    return np.moveaxis((codes * scale).reshape(v.shape), -1, axis)


WIDE = False


def mx_kscale(k):
    if not WIDE:
        return np.ones(k)
    levels = np.array([10, -10, 5, -5, 0])
    a = np.random.permutation(np.resize(levels, k // 512 * 4)).reshape(k // 512, 4)
    idx = np.arange(k)
    return np.exp2(a[idx // 512, idx % 128 // 32])


BF16 = ml_dtypes.bfloat16


def bf(x):
    return np.asarray(x, np.float32).astype(BF16)


def f64(x):
    return np.asarray(x).astype(np.float64)


B, N, P, C, HID, NB, E, MAXLEN = 2, 32, 3, 256, 128, 63, 1024, 2056
F = 3 * HID + 2 * NB + 2
MIN_BIN, MAX_BIN, FAR = 0.001, 20.0, 1e8


def distogram(pos):
    d = np.sqrt(((pos[:, :, None, :] - pos[:, None, :, :]) ** 2).sum(-1))[..., None]
    lower = np.linspace(MIN_BIN, MAX_BIN, NB)
    upper = np.concatenate([lower[1:], [FAR]])
    return np.where((d > lower) & (d < upper), 1.0, 0.0)


def cross_concat(f):
    b, n, d = f.shape
    return np.concatenate([np.broadcast_to(f[:, :, None, :], (b, n, n, d)), np.broadcast_to(f[:, None, :, :], (b, n, n, d))], axis=-1)


def setup_inputs():
    s = np.array(mx_kscale(F))
    s[HID:2 * HID] = s[:HID]
    s[3 * HID:] = 1.0
    sr = s[2 * HID:3 * HID]
    th = np.random.random((B, N, N, HID // 2)) * 2.0 * np.pi
    return {"n2e": bf(np.random.standard_normal((B, N, HID)) * 0.6 * s[:HID]),
            "relpos_emb": bf(np.concatenate([np.sin(th), np.cos(th)], axis=-1)),
            "trans": bf(np.random.standard_normal((B, N, P)) * 10.0),
            "sc_trans": bf(np.random.standard_normal((B, N, P)) * 10.0),
            "flow_mask": bf(np.random.random((B, N)) > 0.5),
            "W_rp": bf(np.random.standard_normal((HID, HID)) * 0.7 / np.sqrt(HID) * sr),
            "b_rp": bf(np.random.standard_normal(HID) * 0.1 * sr),
            "W1": bf(np.random.standard_normal((F, E)) * 2.0 / np.sqrt(F) / s[:, None]),
            "b1": bf(np.random.standard_normal(E) * 0.3)}


def reference(n2e, relpos_emb, trans, sc_trans, flow_mask, W_rp, b_rp, W1, b1):
    pair_node_feats = cross_concat(f64(n2e))
    relpos_feats = f64(relpos_emb) @ f64(W_rp) + f64(b_rp)
    dist_feats = distogram(f64(trans))
    sc_feats = distogram(f64(sc_trans))
    flow_feat = cross_concat(f64(flow_mask)[..., None])
    feats = np.concatenate([pair_node_feats, relpos_feats, dist_feats, sc_feats, flow_feat], axis=-1)
    return np.maximum((mxq(feats, 3, "e4m3") @ mxq(f64(W1), 0, "e4m3")) + f64(b1), 0.0)

@@ -1,0 +1,261 @@
+from contextlib import ExitStack
+
+import concourse.mybir as mybir
+from concourse.masks import make_identity
+
+F32 = mybir.dt.float32
+BF16 = mybir.dt.bfloat16
+U32 = mybir.dt.uint32
+U8 = mybir.dt.uint8
+FP8X4 = mybir.dt.float8_e4m3fn_x4
+ALU = mybir.AluOpType
+ACT = mybir.ActivationFunctionType
+
+BATCH, NODES, XYZ, HID, BINS, WIDTH = 2, 32, 3, 128, 63, 1024
+FEATS = 3 * HID + 2 * BINS + 2
+MIN_BIN, MAX_BIN, FAR = 0.001, 20.0, 1e8
+BIN_STEP = (MAX_BIN - MIN_BIN) / (BINS - 1)
+
+P = 128
+PACK = 4
+PAIRS = BATCH * NODES * NODES
+TILES = PAIRS // P
+HALF = NODES // TILES
+CHUNK = 2
+CHUNKS = TILES // CHUNK
+AHEAD = 2
+N_COLS = 512
+N_HALVES = WIDTH // N_COLS
+
+OWN_TRANS, OWN_SC, OWN_FLOW, OWN_N2E = 0, 16, 32, 48
+OTH_TRANS = OWN_N2E + HID
+OTH_SC = OTH_TRANS + TILES * XYZ
+OTH_FLOW = OTH_SC + TILES * XYZ
+NODE_COLS = OTH_FLOW + TILES
+
+FLOPS = 2 * PAIRS * FEATS * WIDTH + 2 * PAIRS * HID * HID
+
+
+def tile_edgefeaturenet_pa_kernel(
+    tc, n2e, relpos_emb, trans, sc_trans, flow_mask, W_rp, b_rp, W1, b1, out
+):
+    nc = tc.nc
+    with ExitStack() as ctx:
+        const = ctx.enter_context(tc.tile_pool(name="const", bufs=1))
+        work = ctx.enter_context(tc.tile_pool(name="work", bufs=AHEAD + 1))
+        stage = ctx.enter_context(tc.tile_pool(name="stage", bufs=6))
+        psum_small = ctx.enter_context(tc.psum_pool(name="psum_small", bufs=1))
+        psum_words = ctx.enter_context(tc.psum_pool(name="psum_words", bufs=2))
+        psum_acc = ctx.enter_context(tc.psum_pool(name="psum_acc", bufs=4))
+
+        ident_bf = const.tile([P, P], BF16)
+        make_identity(nc, ident_bf[:])
+        bin_index = const.tile([P, BINS + 1], F32)
+        nc.gpsimd.iota(
+            bin_index[:], pattern=[[1, BINS + 1]], base=0, channel_multiplier=0,
+            allow_small_or_imprecise_dtypes=True,
+        )
+        ident_f32 = const.tile([P, P], F32)
+        make_identity(nc, ident_f32[:])
+
+        nodes = const.tile([P, NODE_COLS], BF16)
+        nc.vector.memset(nodes[:], 0.0)
+        others_n2e = const.tile([P, TILES, HID], BF16)
+        nc.vector.memset(others_n2e[:], 0.0)
+        bias_row = const.tile([P, HID], BF16)
+        nc.vector.memset(bias_row[:], 0.0)
+        ones = const.tile([P, P], BF16)
+        nc.vector.memset(ones[:], 1.0)
+
+        with nc.allow_non_contiguous_dma(reason="a few values for each node"):
+            nc.sync.dma_start(out=nodes[0:64, OWN_TRANS:OWN_TRANS + XYZ], in_=trans.rearrange("b n c -> (b n) c"))
+            nc.sync.dma_start(out=nodes[0:64, OWN_SC:OWN_SC + XYZ], in_=sc_trans.rearrange("b n c -> (b n) c"))
+            nc.sync.dma_start(
+                out=nodes[64:68, OTH_TRANS:OTH_SC], in_=trans.rearrange("b (h t) c -> (b h) (t c)", h=HALF)
+            )
+            nc.sync.dma_start(
+                out=nodes[64:68, OTH_SC:OTH_FLOW], in_=sc_trans.rearrange("b (h t) c -> (b h) (t c)", h=HALF)
+            )
+        emb = const.tile([P, TILES, HID], BF16)
+        nc.sync.dma_start(
+            out=emb[:], in_=relpos_emb.rearrange("b i j h -> (b i j) h").rearrange("(p t) h -> p t h", t=TILES)
+        )
+        w_rp = const.tile([P, HID], BF16)
+        nc.sync.dma_start(out=w_rp[:], in_=W_rp)
+        nc.sync.dma_start(out=nodes[0:64, OWN_N2E:OWN_N2E + HID], in_=n2e.rearrange("b n f -> (b n) f"))
+        nc.sync.dma_start(out=others_n2e[64:68, :, :], in_=n2e.rearrange("b (h t) f -> (b h) t f", h=HALF))
+        w_raw = const.tile([P, PACK, WIDTH], BF16)
+        w1_rows = W1.rearrange("(p j) w -> p j w", j=PACK)
+        for n in range(N_HALVES):
+            cols = slice(n * N_COLS, (n + 1) * N_COLS)
+            nc.sync.dma_start(out=w_raw[:, :, cols], in_=w1_rows[:, :, cols])
+        nc.sync.dma_start(out=bias_row[0:1, :], in_=b_rp.rearrange("(o f) -> o f", o=1))
+        with nc.allow_non_contiguous_dma(reason="a few values for each node"):
+            nc.sync.dma_start(
+                out=nodes[0:64, OWN_FLOW:OWN_FLOW + 1], in_=flow_mask.rearrange("b (n o) -> (b n) o", o=1)
+            )
+            nc.sync.dma_start(
+                out=nodes[64:68, OTH_FLOW:NODE_COLS], in_=flow_mask.rearrange("b (h t) -> (b h) t", h=HALF)
+            )
+        bias_all = const.tile([P, WIDTH], BF16)
+        nc.gpsimd.dma_start(out=bias_all[:], in_=b1.partition_broadcast(P))
+
+        edge = const.tile([P, BINS + 1], F32)
+        nc.vector.tensor_scalar(
+            out=edge[:], in0=bin_index[:], scalar1=BIN_STEP, scalar2=MIN_BIN, op0=ALU.mult, op1=ALU.add
+        )
+        edge_sq = const.tile([P, BINS + 1], F32)
+        nc.vector.tensor_tensor(out=edge_sq[:], in0=edge[:], in1=edge[:], op=ALU.mult)
+        nc.vector.memset(edge_sq[:, BINS - 1:BINS], MAX_BIN * MAX_BIN)
+        nc.vector.memset(edge_sq[:, BINS:BINS + 1], FAR * FAR)
+
+        pick = const.tile([P, P], BF16)
+        nc.vector.tensor_tensor(
+            out=pick[:].rearrange("k (b i h) -> k b i h", b=BATCH, h=HALF),
+            in0=ident_bf[:, 0:64].rearrange("k (b i) -> k b i", b=BATCH).unsqueeze(3)
+            .to_broadcast([P, BATCH, NODES, HALF]),
+            in1=ident_bf[:, 64:68].rearrange("k (b h) -> k b h", b=BATCH).unsqueeze(2)
+            .to_broadcast([P, BATCH, NODES, HALF]),
+            op=ALU.add,
+        )
+        spread = psum_words.tile([P, NODE_COLS], F32, tag="words")
+        nc.tensor.matmul(out=spread[:], lhsT=pick[:], rhs=nodes[:], start=True, stop=True)
+
+        own = const.tile([P, OWN_N2E], F32)
+        nc.vector.tensor_copy(out=own[:], in_=spread[:, 0:OWN_N2E])
+        own_n2e = const.tile([P, HID], BF16)
+        nc.scalar.copy(out=own_n2e[:], in_=spread[:, OWN_N2E:OWN_N2E + HID])
+
+        delta = const.tile([P, 2, TILES, XYZ], F32)
+        nc.vector.tensor_tensor(
+            out=delta[:],
+            in0=spread[:, OTH_TRANS:OTH_FLOW].rearrange("p (s t c) -> p s t c", s=2, t=TILES),
+            in1=own[:, 0:OWN_FLOW].rearrange("p (s x) -> p s x", s=2)[:, :, 0:XYZ].unsqueeze(2)
+            .to_broadcast([P, 2, TILES, XYZ]),
+            op=ALU.subtract,
+        )
+        delta_sq = const.tile([P, 2, TILES, XYZ], F32)
+        nc.vector.tensor_tensor(out=delta_sq[:], in0=delta[:], in1=delta[:], op=ALU.mult)
+        dist_sq = const.tile([P, TILES, 2], F32)
+        nc.vector.tensor_reduce(
+            out=dist_sq[:].rearrange("p t s -> p s t"), in_=delta_sq[:], axis=mybir.AxisListType.X, op=ALU.add
+        )
+
+        above = const.tile([P, TILES, HID], BF16)
+        below = const.tile([P, TILES, HID], BF16)
+        nc.vector.tensor_copy(
+            out=above[:, :, HID - 2:HID - 1],
+            in_=spread[:, OWN_FLOW:OWN_FLOW + 1].unsqueeze(1).to_broadcast([P, TILES, 1]),
+        )
+        nc.vector.tensor_copy(out=above[:, :, HID - 1:HID], in_=spread[:, OTH_FLOW:NODE_COLS].unsqueeze(2))
+        nc.vector.memset(below[:, :, HID - 2:HID], 1.0)
+
+        w_codes = const.tile([P, N_HALVES, N_COLS], U32, align_bytes=64)
+        w_scales = const.tile([P, N_HALVES, N_COLS], U8, align_bytes=64)
+        w_grouped = const.tile([P, N_HALVES, N_COLS, PACK], BF16, align_bytes=64)
+
+        def quantise_w1(n):
+            nc.vector.tensor_copy(
+                out=w_grouped[:, n, :, :].rearrange("p (c i) j -> p c j i", i=4),
+                in_=w_raw[:, :, n * N_COLS:(n + 1) * N_COLS].rearrange("p j (c i) -> p c j i", i=4),
+            )
+            nc.vector.quantize_mx(
+                out=w_codes[:, n, :].bitcast(FP8X4),
+                scales=w_scales[:, n, :],
+                in_=w_grouped[:, n, :, :].rearrange("p w j -> p (w j)"),
+            )
+
+        feats_row = const.tile([P, TILES, FEATS], BF16)
+        emb_t = const.tile([P, TILES, P], BF16)
+        f_codes = const.tile([P, CHUNKS, CHUNK * P], U32, align_bytes=64)
+        f_scales = const.tile([P, CHUNKS, CHUNK * P], U8, align_bytes=64)
+        row_words = feats_row[:].bitcast(F32)
+
+        def features(c):
+            tiles = slice(c * CHUNK, (c + 1) * CHUNK)
+            nc.gpsimd.tensor_scalar(
+                out=feats_row[:, tiles, 0:HID], in0=own_n2e[:].unsqueeze(1).to_broadcast([P, CHUNK, HID]),
+                scalar1=1.0, scalar2=0.0, op0=ALU.mult, op1=ALU.add,
+            )
+            emb_t_ps = psum_small.tile([P, CHUNK, P], BF16)
+            for l in range(CHUNK):
+                nc.tensor.transpose(out=emb_t_ps[:, l, :], in_=emb[:, c * CHUNK + l, :], identity=ident_bf[:])
+            nc.scalar.copy(out=emb_t[:, tiles, :], in_=emb_t_ps[:])
+            middle_ps = psum_small.tile([P, CHUNK, 2, HID], F32)
+            for l in range(CHUNK):
+                t = c * CHUNK + l
+                nc.tensor.matmul(out=middle_ps[:, l, 0, :], lhsT=pick[:], rhs=others_n2e[:, t, :], start=True, stop=True)
+                nc.tensor.matmul(out=middle_ps[:, l, 1, :], lhsT=emb_t[:, t, :], rhs=w_rp[:], start=True, stop=False)
+                nc.tensor.matmul(out=middle_ps[:, l, 1, :], lhsT=ones[:], rhs=bias_row[:], start=False, stop=True)
+            nc.scalar.copy(
+                out=feats_row[:, tiles, HID:3 * HID], in_=middle_ps[:].rearrange("p l m f -> p l (m f)")
+            )
+            shape = [P, CHUNK, 2, BINS]
+            d_sq = dist_sq[:, tiles, :].unsqueeze(3).to_broadcast(shape)
+            nc.vector.tensor_tensor(
+                out=above[:, tiles, 0:2 * BINS].rearrange("p t (s k) -> p t s k", s=2),
+                in0=d_sq,
+                in1=edge_sq[:, 0:BINS].unsqueeze(1).unsqueeze(1).to_broadcast(shape),
+                op=ALU.is_gt,
+            )
+            nc.vector.tensor_tensor(
+                out=below[:, tiles, 0:2 * BINS].rearrange("p t (s k) -> p t s k", s=2),
+                in0=d_sq,
+                in1=edge_sq[:, 1:BINS + 1].unsqueeze(1).unsqueeze(1).to_broadcast(shape),
+                op=ALU.is_lt,
+            )
+            nc.gpsimd.tensor_tensor(
+                out=feats_row[:, tiles, 3 * HID:FEATS], in0=above[:, tiles, :], in1=below[:, tiles, :], op=ALU.mult
+            )
+            grouped = work.tile([P, CHUNK, P, PACK], BF16, align_bytes=64)
+            words_ps = psum_words.tile([P, CHUNK, 2, P], F32, tag="words")
+            for l in range(CHUNK):
+                for u in range(2):
+                    nc.tensor.transpose(
+                        out=words_ps[:, l, u, :],
+                        in_=row_words[:, c * CHUNK + l, u:FEATS // 2:2],
+                        identity=ident_f32[:],
+                    )
+            nc.scalar.copy(out=grouped[:].bitcast(F32), in_=words_ps[:].rearrange("p l u r -> p l r u"))
+            nc.vector.quantize_mx(
+                out=f_codes[:, c, :].bitcast(FP8X4),
+                scales=f_scales[:, c, :],
+                in_=grouped[:].rearrange("p l r j -> p (l r j)"),
+            )
+
+        out_rows = out.rearrange("b i j e -> (b i j) e").rearrange("(p t) e -> p t e", t=TILES)
+
+        def layer(c):
+            for l in range(CHUNK):
+                pairs = slice(l * P, (l + 1) * P)
+                result = stage.tile([P, WIDTH], F32)
+                for n in range(N_HALVES):
+                    cols = slice(n * N_COLS, (n + 1) * N_COLS)
+                    acc = psum_acc.tile([P, N_COLS], F32)
+                    nc.tensor.matmul_mx(
+                        out=acc[:],
+                        lhsT=f_codes[:, c, pairs].bitcast(FP8X4),
+                        lhsT_scale=f_scales[:, c, pairs],
+                        rhs=w_codes[:, n, :].bitcast(FP8X4),
+                        rhs_scale=w_scales[:, n, :],
+                        start=True,
+                        stop=True,
+                    )
+                    nc.vector.tensor_tensor(out=result[:, cols], in0=acc[:], in1=bias_all[:, cols], op=ALU.add)
+                if l % 2 == 0:
+                    nc.scalar.activation(out=result[:], in_=result[:], func=ACT.Relu)
+                else:
+                    nc.gpsimd.tensor_scalar(
+                        out=result[:], in0=result[:], scalar1=float("inf"), scalar2=0.0, op0=ALU.min, op1=ALU.max
+                    )
+                nc.sync.dma_start(out=out_rows[:, c * CHUNK + l, :], in_=result[:])
+
+        features(0)
+        for n in range(N_HALVES):
+            quantise_w1(n)
+        for c in range(1, AHEAD):
+            features(c)
+        for c in range(CHUNKS):
+            if c + AHEAD < CHUNKS:
+                features(c + AHEAD)
+            layer(c)

@@ -154,11 +154,16 @@ def tile_edgefeaturenet_pa_kernel(
         w_scales = const.tile([P, N_HALVES, N_COLS], U8, align_bytes=64)
         w_grouped = const.tile([P, N_HALVES, N_COLS, PACK], BF16, align_bytes=64)
 
-        def quantise_w1(n):
-            nc.vector.tensor_copy(
+        def regrouped(n):
+            return dict(
                 out=w_grouped[:, n, :, :].rearrange("p (c i) j -> p c j i", i=4),
                 in_=w_raw[:, :, n * N_COLS:(n + 1) * N_COLS].rearrange("p j (c i) -> p c j i", i=4),
             )
+
+        nc.vector.tensor_copy(**regrouped(0))
+        nc.scalar.copy(**regrouped(1))
+
+        def quantise_w1(n):
             nc.vector.quantize_mx(
                 out=w_codes[:, n, :].bitcast(FP8X4),
                 scales=w_scales[:, n, :],
@@ -173,9 +178,8 @@ def tile_edgefeaturenet_pa_kernel(
 
         def features(c):
             tiles = slice(c * CHUNK, (c + 1) * CHUNK)
-            nc.gpsimd.tensor_scalar(
-                out=feats_row[:, tiles, 0:HID], in0=own_n2e[:].unsqueeze(1).to_broadcast([P, CHUNK, HID]),
-                scalar1=1.0, scalar2=0.0, op0=ALU.mult, op1=ALU.add,
+            nc.vector.tensor_copy(
+                out=feats_row[:, tiles, 0:HID], in_=own_n2e[:].unsqueeze(1).to_broadcast([P, CHUNK, HID])
             )
             emb_t_ps = psum_small.tile([P, CHUNK, P], BF16)
             for l in range(CHUNK):
@@ -204,7 +208,7 @@ def tile_edgefeaturenet_pa_kernel(
                 in1=edge_sq[:, 1:BINS + 1].unsqueeze(1).unsqueeze(1).to_broadcast(shape),
                 op=ALU.is_lt,
             )
-            nc.gpsimd.tensor_tensor(
+            nc.vector.tensor_tensor(
                 out=feats_row[:, tiles, 3 * HID:FEATS], in0=above[:, tiles, :], in1=below[:, tiles, :], op=ALU.mult
             )
             grouped = work.tile([P, CHUNK, P, PACK], BF16, align_bytes=64)
@@ -242,12 +246,7 @@ def tile_edgefeaturenet_pa_kernel(
                         stop=True,
                     )
                     nc.vector.tensor_tensor(out=result[:, cols], in0=acc[:], in1=bias_all[:, cols], op=ALU.add)
-                if l % 2 == 0:
-                    nc.scalar.activation(out=result[:], in_=result[:], func=ACT.Relu)
-                else:
-                    nc.gpsimd.tensor_scalar(
-                        out=result[:], in0=result[:], scalar1=float("inf"), scalar2=0.0, op0=ALU.min, op1=ALU.max
-                    )
+                nc.scalar.activation(out=result[:], in_=result[:], func=ACT.Relu)
                 nc.sync.dma_start(out=out_rows[:, c * CHUNK + l, :], in_=result[:])
 
         features(0)

@@ -23,15 +23,14 @@ TILES = PAIRS // P
 HALF = NODES // TILES
 CHUNK = 2
 CHUNKS = TILES // CHUNK
-AHEAD = 2
 N_COLS = 512
 N_HALVES = WIDTH // N_COLS
 
-OWN_TRANS, OWN_SC, OWN_FLOW, OWN_N2E = 0, 16, 32, 48
-OTH_TRANS = OWN_N2E + HID
+OWN_TRANS, OWN_SC, OTH_TRANS = 0, 16, 32
 OTH_SC = OTH_TRANS + TILES * XYZ
-OTH_FLOW = OTH_SC + TILES * XYZ
-NODE_COLS = OTH_FLOW + TILES
+OWN_N2E = OTH_SC + TILES * XYZ
+POS_COLS = OWN_N2E + HID
+OWN_FLOW, OTH_FLOW, FLOW_COLS = 0, 16, 32
 
 FLOPS = 2 * PAIRS * FEATS * WIDTH + 2 * PAIRS * HID * HID
 
@@ -41,10 +40,11 @@ def tile_edgefeaturenet_pa_kernel(
 ):
     nc = tc.nc
     with ExitStack() as ctx:
+        ctx.enter_context(tc.manual_schedule())
         const = ctx.enter_context(tc.tile_pool(name="const", bufs=1))
-        work = ctx.enter_context(tc.tile_pool(name="work", bufs=AHEAD + 1))
+        work = ctx.enter_context(tc.tile_pool(name="work", bufs=3))
         stage = ctx.enter_context(tc.tile_pool(name="stage", bufs=6))
-        psum_small = ctx.enter_context(tc.psum_pool(name="psum_small", bufs=1))
+        psum_middle = ctx.enter_context(tc.psum_pool(name="psum_middle", bufs=2))
         psum_words = ctx.enter_context(tc.psum_pool(name="psum_words", bufs=2))
         psum_acc = ctx.enter_context(tc.psum_pool(name="psum_acc", bufs=4))
 
@@ -58,8 +58,10 @@ def tile_edgefeaturenet_pa_kernel(
         ident_f32 = const.tile([P, P], F32)
         make_identity(nc, ident_f32[:])
 
-        nodes = const.tile([P, NODE_COLS], BF16)
-        nc.vector.memset(nodes[:], 0.0)
+        node_pos = const.tile([P, POS_COLS], BF16)
+        nc.vector.memset(node_pos[:], 0.0)
+        node_flow = const.tile([P, FLOW_COLS], BF16)
+        nc.vector.memset(node_flow[:], 0.0)
         others_n2e = const.tile([P, TILES, HID], BF16)
         nc.vector.memset(others_n2e[:], 0.0)
         bias_row = const.tile([P, HID], BF16)
@@ -67,36 +69,36 @@ def tile_edgefeaturenet_pa_kernel(
         ones = const.tile([P, P], BF16)
         nc.vector.memset(ones[:], 1.0)
 
-        with nc.allow_non_contiguous_dma(reason="a few values for each node"):
-            nc.sync.dma_start(out=nodes[0:64, OWN_TRANS:OWN_TRANS + XYZ], in_=trans.rearrange("b n c -> (b n) c"))
-            nc.sync.dma_start(out=nodes[0:64, OWN_SC:OWN_SC + XYZ], in_=sc_trans.rearrange("b n c -> (b n) c"))
-            nc.sync.dma_start(
-                out=nodes[64:68, OTH_TRANS:OTH_SC], in_=trans.rearrange("b (h t) c -> (b h) (t c)", h=HALF)
-            )
-            nc.sync.dma_start(
-                out=nodes[64:68, OTH_SC:OTH_FLOW], in_=sc_trans.rearrange("b (h t) c -> (b h) (t c)", h=HALF)
-            )
+        with nc.allow_non_contiguous_dma(reason="three values for each node"):
+            nc.sync.dma_start(out=node_pos[0:64, OWN_TRANS:OWN_TRANS + XYZ], in_=trans.rearrange("b n c -> (b n) c"))
+            nc.sync.dma_start(out=node_pos[0:64, OWN_SC:OWN_SC + XYZ], in_=sc_trans.rearrange("b n c -> (b n) c"))
+        nc.sync.dma_start(
+            out=node_pos[64:68, OTH_TRANS:OTH_SC], in_=trans.rearrange("b (h t) c -> (b h) (t c)", h=HALF)
+        )
+        nc.sync.dma_start(
+            out=node_pos[64:68, OTH_SC:OWN_N2E], in_=sc_trans.rearrange("b (h t) c -> (b h) (t c)", h=HALF)
+        )
+        nc.sync.dma_start(out=node_pos[0:64, OWN_N2E:POS_COLS], in_=n2e.rearrange("b n f -> (b n) f"))
         emb = const.tile([P, TILES, HID], BF16)
         nc.sync.dma_start(
             out=emb[:], in_=relpos_emb.rearrange("b i j h -> (b i j) h").rearrange("(p t) h -> p t h", t=TILES)
         )
-        w_rp = const.tile([P, HID], BF16)
-        nc.sync.dma_start(out=w_rp[:], in_=W_rp)
-        nc.sync.dma_start(out=nodes[0:64, OWN_N2E:OWN_N2E + HID], in_=n2e.rearrange("b n f -> (b n) f"))
-        nc.sync.dma_start(out=others_n2e[64:68, :, :], in_=n2e.rearrange("b (h t) f -> (b h) t f", h=HALF))
         w_raw = const.tile([P, PACK, WIDTH], BF16)
         w1_rows = W1.rearrange("(p j) w -> p j w", j=PACK)
         for n in range(N_HALVES):
             cols = slice(n * N_COLS, (n + 1) * N_COLS)
             nc.sync.dma_start(out=w_raw[:, :, cols], in_=w1_rows[:, :, cols])
+        w_rp = const.tile([P, HID], BF16)
+        nc.sync.dma_start(out=w_rp[:], in_=W_rp)
+        nc.sync.dma_start(out=others_n2e[64:68, :, :], in_=n2e.rearrange("b (h t) f -> (b h) t f", h=HALF))
         nc.sync.dma_start(out=bias_row[0:1, :], in_=b_rp.rearrange("(o f) -> o f", o=1))
-        with nc.allow_non_contiguous_dma(reason="a few values for each node"):
+        with nc.allow_non_contiguous_dma(reason="one value for each node"):
             nc.sync.dma_start(
-                out=nodes[0:64, OWN_FLOW:OWN_FLOW + 1], in_=flow_mask.rearrange("b (n o) -> (b n) o", o=1)
+                out=node_flow[0:64, OWN_FLOW:OWN_FLOW + 1], in_=flow_mask.rearrange("b (n o) -> (b n) o", o=1)
             )
-            nc.sync.dma_start(
-                out=nodes[64:68, OTH_FLOW:NODE_COLS], in_=flow_mask.rearrange("b (h t) -> (b h) t", h=HALF)
-            )
+        nc.sync.dma_start(
+            out=node_flow[64:68, OTH_FLOW:FLOW_COLS], in_=flow_mask.rearrange("b (h t) -> (b h) t", h=HALF)
+        )
         bias_all = const.tile([P, WIDTH], BF16)
         nc.gpsimd.dma_start(out=bias_all[:], in_=b1.partition_broadcast(P))
 
@@ -118,143 +120,189 @@ def tile_edgefeaturenet_pa_kernel(
             .to_broadcast([P, BATCH, NODES, HALF]),
             op=ALU.add,
         )
-        spread = psum_words.tile([P, NODE_COLS], F32, tag="words")
-        nc.tensor.matmul(out=spread[:], lhsT=pick[:], rhs=nodes[:], start=True, stop=True)
+        pos_ps = psum_words.tile([P, POS_COLS], F32, tag="words")
+        nc.tensor.matmul(out=pos_ps[:], lhsT=pick[:], rhs=node_pos[:], start=True, stop=True)
 
-        own = const.tile([P, OWN_N2E], F32)
-        nc.vector.tensor_copy(out=own[:], in_=spread[:, 0:OWN_N2E])
-        own_n2e = const.tile([P, HID], BF16)
-        nc.scalar.copy(out=own_n2e[:], in_=spread[:, OWN_N2E:OWN_N2E + HID])
-
+        own_pos = const.tile([P, OTH_TRANS], F32)
+        nc.vector.tensor_copy(out=own_pos[:], in_=pos_ps[:, 0:OTH_TRANS])
         delta = const.tile([P, 2, TILES, XYZ], F32)
         nc.vector.tensor_tensor(
             out=delta[:],
-            in0=spread[:, OTH_TRANS:OTH_FLOW].rearrange("p (s t c) -> p s t c", s=2, t=TILES),
-            in1=own[:, 0:OWN_FLOW].rearrange("p (s x) -> p s x", s=2)[:, :, 0:XYZ].unsqueeze(2)
+            in0=pos_ps[:, OTH_TRANS:OWN_N2E].rearrange("p (s t c) -> p s t c", s=2, t=TILES),
+            in1=own_pos[:].rearrange("p (s x) -> p s x", s=2)[:, :, 0:XYZ].unsqueeze(2)
             .to_broadcast([P, 2, TILES, XYZ]),
             op=ALU.subtract,
         )
         delta_sq = const.tile([P, 2, TILES, XYZ], F32)
         nc.vector.tensor_tensor(out=delta_sq[:], in0=delta[:], in1=delta[:], op=ALU.mult)
-        dist_sq = const.tile([P, TILES, 2], F32)
+        raw_sq = const.tile([P, TILES, 2], F32)
         nc.vector.tensor_reduce(
-            out=dist_sq[:].rearrange("p t s -> p s t"), in_=delta_sq[:], axis=mybir.AxisListType.X, op=ALU.add
+            out=raw_sq[:].rearrange("p t s -> p s t"), in_=delta_sq[:], axis=mybir.AxisListType.X, op=ALU.add
+        )
+        dist_sq = const.tile([P, TILES, 2], F32)
+        nc.vector.scalar_tensor_tensor(
+            out=dist_sq[:].rearrange("p t s -> p (t s)"), in0=raw_sq[:].rearrange("p t s -> p (t s)"),
+            scalar=MAX_BIN * MAX_BIN, in1=raw_sq[:].rearrange("p t s -> p (t s)"),
+            op0=ALU.not_equal, op1=ALU.mult,
         )
 
-        above = const.tile([P, TILES, HID], BF16)
-        below = const.tile([P, TILES, HID], BF16)
-        nc.vector.tensor_copy(
-            out=above[:, :, HID - 2:HID - 1],
-            in_=spread[:, OWN_FLOW:OWN_FLOW + 1].unsqueeze(1).to_broadcast([P, TILES, 1]),
+        own_n2e = const.tile([P, HID], BF16)
+        nc.scalar.copy(out=own_n2e[:], in_=pos_ps[:, OWN_N2E:POS_COLS])
+
+        emb_t = const.tile([P, TILES, P], BF16)
+        for half in range(2):
+            tiles = slice(half * TILES // 2, (half + 1) * TILES // 2)
+            emb_t_ps = psum_acc.tile([P, TILES // 2, P], BF16, tag="acc")
+            for l in range(TILES // 2):
+                nc.tensor.transpose(out=emb_t_ps[:, l, :], in_=emb[:, half * TILES // 2 + l, :], identity=ident_bf[:])
+            nc.scalar.copy(out=emb_t[:, tiles, :], in_=emb_t_ps[:])
+
+        flow_ps = psum_words.tile([P, FLOW_COLS], F32, tag="words")
+        nc.tensor.matmul(out=flow_ps[:], lhsT=pick[:], rhs=node_flow[:], start=True, stop=True)
+        flags = const.tile([P, TILES, 2], BF16)
+        nc.scalar.copy(
+            out=flags[:, :, 0:1], in_=flow_ps[:, OWN_FLOW:OWN_FLOW + 1].unsqueeze(1).to_broadcast([P, TILES, 1])
         )
-        nc.vector.tensor_copy(out=above[:, :, HID - 1:HID], in_=spread[:, OTH_FLOW:NODE_COLS].unsqueeze(2))
-        nc.vector.memset(below[:, :, HID - 2:HID], 1.0)
-
-        w_codes = const.tile([P, N_HALVES, N_COLS], U32, align_bytes=64)
-        w_scales = const.tile([P, N_HALVES, N_COLS], U8, align_bytes=64)
-        w_grouped = const.tile([P, N_HALVES, N_COLS, PACK], BF16, align_bytes=64)
-
-        def regrouped(n):
-            return dict(
-                out=w_grouped[:, n, :, :].rearrange("p (c i) j -> p c j i", i=4),
-                in_=w_raw[:, :, n * N_COLS:(n + 1) * N_COLS].rearrange("p j (c i) -> p c j i", i=4),
-            )
-
-        nc.vector.tensor_copy(**regrouped(0))
-        nc.scalar.copy(**regrouped(1))
-
-        def quantise_w1(n):
-            nc.vector.quantize_mx(
-                out=w_codes[:, n, :].bitcast(FP8X4),
-                scales=w_scales[:, n, :],
-                in_=w_grouped[:, n, :, :].rearrange("p w j -> p (w j)"),
-            )
+        nc.scalar.copy(out=flags[:, :, 1:2], in_=flow_ps[:, OTH_FLOW:FLOW_COLS].unsqueeze(2))
 
         feats_row = const.tile([P, TILES, FEATS], BF16)
-        emb_t = const.tile([P, TILES, P], BF16)
+        row_words = feats_row[:].bitcast(F32)
+        above = const.tile([P, TILES, 2, BINS + 1], BF16)
+        w_codes = const.tile([P, N_HALVES, N_COLS], U32, align_bytes=64)
+        w_scales = const.tile([P, N_HALVES, N_COLS], U8, align_bytes=64)
         f_codes = const.tile([P, CHUNKS, CHUNK * P], U32, align_bytes=64)
         f_scales = const.tile([P, CHUNKS, CHUNK * P], U8, align_bytes=64)
-        row_words = feats_row[:].bitcast(F32)
+        out_rows = out.rearrange("b i j e -> (b i j) e").rearrange("(p t) e -> p t e", t=TILES)
+        middle_ps, words_ps, grouped, acc, result = {}, {}, {}, {}, {}
 
-        def features(c):
-            tiles = slice(c * CHUNK, (c + 1) * CHUNK)
-            nc.vector.tensor_copy(
-                out=feats_row[:, tiles, 0:HID], in_=own_n2e[:].unsqueeze(1).to_broadcast([P, CHUNK, HID])
-            )
-            emb_t_ps = psum_small.tile([P, CHUNK, P], BF16)
-            for l in range(CHUNK):
-                nc.tensor.transpose(out=emb_t_ps[:, l, :], in_=emb[:, c * CHUNK + l, :], identity=ident_bf[:])
-            nc.scalar.copy(out=emb_t[:, tiles, :], in_=emb_t_ps[:])
-            middle_ps = psum_small.tile([P, CHUNK, 2, HID], F32)
-            for l in range(CHUNK):
-                t = c * CHUNK + l
-                nc.tensor.matmul(out=middle_ps[:, l, 0, :], lhsT=pick[:], rhs=others_n2e[:, t, :], start=True, stop=True)
-                nc.tensor.matmul(out=middle_ps[:, l, 1, :], lhsT=emb_t[:, t, :], rhs=w_rp[:], start=True, stop=False)
-                nc.tensor.matmul(out=middle_ps[:, l, 1, :], lhsT=ones[:], rhs=bias_row[:], start=False, stop=True)
-            nc.scalar.copy(
-                out=feats_row[:, tiles, HID:3 * HID], in_=middle_ps[:].rearrange("p l m f -> p l (m f)")
-            )
-            shape = [P, CHUNK, 2, BINS]
-            d_sq = dist_sq[:, tiles, :].unsqueeze(3).to_broadcast(shape)
+        def tiles_of(c):
+            return slice(c * CHUNK, (c + 1) * CHUNK)
+
+        def compare(c):
+            shape = [P, CHUNK * 2, BINS + 1]
             nc.vector.tensor_tensor(
-                out=above[:, tiles, 0:2 * BINS].rearrange("p t (s k) -> p t s k", s=2),
-                in0=d_sq,
-                in1=edge_sq[:, 0:BINS].unsqueeze(1).unsqueeze(1).to_broadcast(shape),
+                out=above[:, tiles_of(c), :, :].rearrange("p t s k -> p (t s) k"),
+                in0=dist_sq[:, tiles_of(c), :].rearrange("p t s -> p (t s)").unsqueeze(2).to_broadcast(shape),
+                in1=edge_sq[:].unsqueeze(1).to_broadcast(shape),
                 op=ALU.is_gt,
             )
-            nc.vector.tensor_tensor(
-                out=below[:, tiles, 0:2 * BINS].rearrange("p t (s k) -> p t s k", s=2),
-                in0=d_sq,
-                in1=edge_sq[:, 1:BINS + 1].unsqueeze(1).unsqueeze(1).to_broadcast(shape),
-                op=ALU.is_lt,
+
+        def outer_features(c):
+            nc.gpsimd.tensor_scalar(
+                out=feats_row[:, tiles_of(c), 0:HID], in0=own_n2e[:].unsqueeze(1).to_broadcast([P, CHUNK, HID]),
+                scalar1=1.0, scalar2=0.0, op0=ALU.mult, op1=ALU.add,
             )
-            nc.vector.tensor_tensor(
-                out=feats_row[:, tiles, 3 * HID:FEATS], in0=above[:, tiles, :], in1=below[:, tiles, :], op=ALU.mult
+            nc.gpsimd.tensor_tensor(
+                out=feats_row[:, tiles_of(c), 3 * HID:3 * HID + 2 * BINS].rearrange("p t (s k) -> p t s k", s=2),
+                in0=above[:, tiles_of(c), :, 0:BINS],
+                in1=above[:, tiles_of(c), :, 1:BINS + 1],
+                op=ALU.subtract,
             )
-            grouped = work.tile([P, CHUNK, P, PACK], BF16, align_bytes=64)
-            words_ps = psum_words.tile([P, CHUNK, 2, P], F32, tag="words")
+            nc.gpsimd.tensor_scalar(
+                out=feats_row[:, tiles_of(c), FEATS - 2:FEATS], in0=flags[:, tiles_of(c), :],
+                scalar1=1.0, scalar2=0.0, op0=ALU.mult, op1=ALU.add,
+            )
+
+        def middle_matmuls(c):
+            middle_ps[c] = psum_middle.tile([P, CHUNK, 2, HID], F32, name="middle_ps")
+            for l in range(CHUNK):
+                t = c * CHUNK + l
+                nc.tensor.matmul(
+                    out=middle_ps[c][:, l, 0, :], lhsT=pick[:], rhs=others_n2e[:, t, :], start=True, stop=True
+                )
+                nc.tensor.matmul(out=middle_ps[c][:, l, 1, :], lhsT=emb_t[:, t, :], rhs=w_rp[:], start=True, stop=False)
+                nc.tensor.matmul(out=middle_ps[c][:, l, 1, :], lhsT=ones[:], rhs=bias_row[:], start=False, stop=True)
+
+        def middle_features(c):
+            nc.scalar.copy(
+                out=feats_row[:, tiles_of(c), HID:3 * HID], in_=middle_ps[c][:].rearrange("p l m f -> p l (m f)")
+            )
+
+        def transpose_words(c):
+            words_ps[c] = psum_words.tile([P, CHUNK, 2, P], F32, name="words_ps", tag="words")
             for l in range(CHUNK):
                 for u in range(2):
                     nc.tensor.transpose(
-                        out=words_ps[:, l, u, :],
+                        out=words_ps[c][:, l, u, :],
                         in_=row_words[:, c * CHUNK + l, u:FEATS // 2:2],
                         identity=ident_f32[:],
                     )
-            nc.scalar.copy(out=grouped[:].bitcast(F32), in_=words_ps[:].rearrange("p l u r -> p l r u"))
+
+        def group_words(c):
+            grouped[c] = work.tile([P, CHUNK, P, PACK], BF16, name="grouped", align_bytes=64)
+            nc.scalar.copy(out=grouped[c][:].bitcast(F32), in_=words_ps[c][:].rearrange("p l u r -> p l r u"))
+
+        def quantise_features(c):
             nc.vector.quantize_mx(
                 out=f_codes[:, c, :].bitcast(FP8X4),
                 scales=f_scales[:, c, :],
-                in_=grouped[:].rearrange("p l r j -> p (l r j)"),
+                in_=grouped[c][:].rearrange("p l r j -> p (l r j)"),
             )
 
-        out_rows = out.rearrange("b i j e -> (b i j) e").rearrange("(p t) e -> p t e", t=TILES)
+        def quantise_w1(n):
+            w_grouped = work.tile([P, N_COLS, PACK], BF16, align_bytes=64)
+            nc.vector.tensor_copy(
+                out=w_grouped[:].rearrange("p (c i) j -> p c j i", i=4),
+                in_=w_raw[:, :, n * N_COLS:(n + 1) * N_COLS].rearrange("p j (c i) -> p c j i", i=4),
+            )
+            nc.vector.quantize_mx(
+                out=w_codes[:, n, :].bitcast(FP8X4), scales=w_scales[:, n, :],
+                in_=w_grouped[:].rearrange("p w j -> p (w j)"),
+            )
 
-        def layer(c):
+        def passes(c):
             for l in range(CHUNK):
-                pairs = slice(l * P, (l + 1) * P)
-                result = stage.tile([P, WIDTH], F32)
                 for n in range(N_HALVES):
-                    cols = slice(n * N_COLS, (n + 1) * N_COLS)
-                    acc = psum_acc.tile([P, N_COLS], F32)
+                    acc[c, l, n] = psum_acc.tile([P, N_COLS], F32, name="acc", tag="acc")
                     nc.tensor.matmul_mx(
-                        out=acc[:],
-                        lhsT=f_codes[:, c, pairs].bitcast(FP8X4),
-                        lhsT_scale=f_scales[:, c, pairs],
+                        out=acc[c, l, n][:],
+                        lhsT=f_codes[:, c, l * P:(l + 1) * P].bitcast(FP8X4),
+                        lhsT_scale=f_scales[:, c, l * P:(l + 1) * P],
                         rhs=w_codes[:, n, :].bitcast(FP8X4),
                         rhs_scale=w_scales[:, n, :],
                         start=True,
                         stop=True,
                     )
-                    nc.vector.tensor_tensor(out=result[:, cols], in0=acc[:], in1=bias_all[:, cols], op=ALU.add)
-                nc.scalar.activation(out=result[:], in_=result[:], func=ACT.Relu)
-                nc.sync.dma_start(out=out_rows[:, c * CHUNK + l, :], in_=result[:])
 
-        features(0)
-        for n in range(N_HALVES):
-            quantise_w1(n)
-        for c in range(1, AHEAD):
-            features(c)
-        for c in range(CHUNKS):
-            if c + AHEAD < CHUNKS:
-                features(c + AHEAD)
-            layer(c)
+        def add_bias(c):
+            for l in range(CHUNK):
+                result[c, l] = stage.tile([P, WIDTH], F32, name="result")
+                for n in range(N_HALVES):
+                    cols = slice(n * N_COLS, (n + 1) * N_COLS)
+                    nc.vector.tensor_tensor(
+                        out=result[c, l][:, cols], in0=acc[c, l, n][:], in1=bias_all[:, cols], op=ALU.add
+                    )
+
+        def relu_and_store(c, l):
+            nc.scalar.activation(out=result[c, l][:], in_=result[c, l][:], func=ACT.Relu)
+            nc.sync.dma_start(out=out_rows[:, c * CHUNK + l, :], in_=result[c, l][:])
+
+        def live(c):
+            return 0 <= c < CHUNKS
+
+        for s in range(-5, CHUNKS + 1):
+            if s == -1:
+                for n in range(N_HALVES):
+                    quantise_w1(n)
+            if live(s + 1):
+                quantise_features(s + 1)
+            if live(s):
+                add_bias(s)
+            if live(s + 5):
+                compare(s + 5)
+            if live(s + 4):
+                outer_features(s + 4)
+            if live(s + 3):
+                transpose_words(s + 3)
+            if live(s + 5):
+                middle_matmuls(s + 5)
+            if live(s + 1):
+                passes(s + 1)
+            if live(s - 1):
+                relu_and_store(s - 1, 1)
+            if live(s + 2):
+                group_words(s + 2)
+            if live(s + 4):
+                middle_features(s + 4)
+            if live(s):
+                relu_and_store(s, 0)

@@ -23,6 +23,7 @@ TILES = PAIRS // P
 HALF = NODES // TILES
 CHUNK = 2
 CHUNKS = TILES // CHUNK
+COMPARED = 2
 N_COLS = 512
 N_HALVES = WIDTH // N_COLS
 
@@ -100,7 +101,7 @@ def tile_edgefeaturenet_pa_kernel(
             out=node_flow[64:68, OTH_FLOW:FLOW_COLS], in_=flow_mask.rearrange("b (h t) -> (b h) t", h=HALF)
         )
         bias_all = const.tile([P, WIDTH], BF16)
-        nc.gpsimd.dma_start(out=bias_all[:], in_=b1.partition_broadcast(P))
+        nc.sync.dma_start(out=bias_all[:], in_=b1.partition_broadcast(P))
 
         edge = const.tile([P, BINS + 1], F32)
         nc.vector.tensor_scalar(
@@ -179,10 +180,11 @@ def tile_edgefeaturenet_pa_kernel(
             return slice(c * CHUNK, (c + 1) * CHUNK)
 
         def compare(c):
-            shape = [P, CHUNK * 2, BINS + 1]
+            tiles = slice(c * CHUNK, (c + COMPARED) * CHUNK)
+            shape = [P, COMPARED * CHUNK * 2, BINS + 1]
             nc.vector.tensor_tensor(
-                out=above[:, tiles_of(c), :, :].rearrange("p t s k -> p (t s) k"),
-                in0=dist_sq[:, tiles_of(c), :].rearrange("p t s -> p (t s)").unsqueeze(2).to_broadcast(shape),
+                out=above[:, tiles, :, :].rearrange("p t s k -> p (t s) k"),
+                in0=dist_sq[:, tiles, :].rearrange("p t s -> p (t s)").unsqueeze(2).to_broadcast(shape),
                 in1=edge_sq[:].unsqueeze(1).to_broadcast(shape),
                 op=ALU.is_gt,
             )
@@ -274,8 +276,12 @@ def tile_edgefeaturenet_pa_kernel(
                     )
 
         def relu_and_store(c, l):
-            nc.scalar.activation(out=result[c, l][:], in_=result[c, l][:], func=ACT.Relu)
-            nc.sync.dma_start(out=out_rows[:, c * CHUNK + l, :], in_=result[c, l][:])
+            last = c == CHUNKS - 1 and l == CHUNK - 1
+            width = N_COLS if last else WIDTH
+            for first in range(0, WIDTH, width):
+                cols = slice(first, first + width)
+                nc.scalar.activation(out=result[c, l][:, cols], in_=result[c, l][:, cols], func=ACT.Relu)
+                nc.sync.dma_start(out=out_rows[:, c * CHUNK + l, cols], in_=result[c, l][:, cols])
 
         def live(c):
             return 0 <= c < CHUNKS
@@ -288,7 +294,7 @@ def tile_edgefeaturenet_pa_kernel(
                 quantise_features(s + 1)
             if live(s):
                 add_bias(s)
-            if live(s + 5):
+            if live(s + 5) and (s + 5) % COMPARED == 0:
                 compare(s + 5)
             if live(s + 4):
                 outer_features(s + 4)

@@ -26,6 +26,7 @@ CHUNKS = TILES // CHUNK
 COMPARED = 2
 N_COLS = 512
 N_HALVES = WIDTH // N_COLS
+SHARED_RELUS = (0, 2, 3)
 
 OWN_TRANS, OWN_SC, OTH_TRANS = 0, 16, 32
 OTH_SC = OTH_TRANS + TILES * XYZ
@@ -276,6 +277,13 @@ def tile_edgefeaturenet_pa_kernel(
                     )
 
         def relu_and_store(c, l):
+            if l == 0 and c in SHARED_RELUS:
+                nc.scalar.activation(out=result[c, l][:, 0:N_COLS], in_=result[c, l][:, 0:N_COLS], func=ACT.Relu)
+                nc.vector.tensor_scalar_max(
+                    out=result[c, l][:, N_COLS:WIDTH], in0=result[c, l][:, N_COLS:WIDTH], scalar1=0.0
+                )
+                nc.sync.dma_start(out=out_rows[:, c * CHUNK + l, :], in_=result[c, l][:])
+                return
             last = c == CHUNKS - 1 and l == CHUNK - 1
             width = N_COLS if last else WIDTH
             for first in range(0, WIDTH, width):

@@ -176,6 +176,7 @@ def tile_edgefeaturenet_pa_kernel(
         f_scales = const.tile([P, CHUNKS, CHUNK * P], U8, align_bytes=64)
         out_rows = out.rearrange("b i j e -> (b i j) e").rearrange("(p t) e -> p t e", t=TILES)
         middle_ps, words_ps, grouped, acc, result = {}, {}, {}, {}, {}
+        relpos_ps, others_ps = {}, {}
 
         def tiles_of(c):
             return slice(c * CHUNK, (c + 1) * CHUNK)
@@ -207,19 +208,21 @@ def tile_edgefeaturenet_pa_kernel(
             )
 
         def middle_matmuls(c):
-            middle_ps[c] = psum_middle.tile([P, CHUNK, 2, HID], F32, name="middle_ps")
+            middle_ps[c] = psum_middle.tile([P, 2 * CHUNK * HID], F32, name="middle_ps")
+            relpos_ps[c] = middle_ps[c][:, 0:CHUNK * HID].rearrange("p (l f) -> p l f", l=CHUNK)
+            others_ps[c] = (
+                middle_ps[c][:, CHUNK * HID:CHUNK * HID + CHUNK * HID // 2].bitcast(BF16)
+                .rearrange("p (l f) -> p l f", l=CHUNK)
+            )
             for l in range(CHUNK):
                 t = c * CHUNK + l
-                nc.tensor.matmul(
-                    out=middle_ps[c][:, l, 0, :], lhsT=pick[:], rhs=others_n2e[:, t, :], start=True, stop=True
-                )
-                nc.tensor.matmul(out=middle_ps[c][:, l, 1, :], lhsT=emb_t[:, t, :], rhs=w_rp[:], start=True, stop=False)
-                nc.tensor.matmul(out=middle_ps[c][:, l, 1, :], lhsT=ones[:], rhs=bias_row[:], start=False, stop=True)
+                nc.tensor.matmul(out=others_ps[c][:, l, :], lhsT=pick[:], rhs=others_n2e[:, t, :], start=True, stop=True)
+                nc.tensor.matmul(out=relpos_ps[c][:, l, :], lhsT=emb_t[:, t, :], rhs=w_rp[:], start=True, stop=False)
+                nc.tensor.matmul(out=relpos_ps[c][:, l, :], lhsT=ones[:], rhs=bias_row[:], start=False, stop=True)
 
         def middle_features(c):
-            nc.scalar.copy(
-                out=feats_row[:, tiles_of(c), HID:3 * HID], in_=middle_ps[c][:].rearrange("p l m f -> p l (m f)")
-            )
+            nc.scalar.copy(out=feats_row[:, tiles_of(c), HID:2 * HID], in_=others_ps[c])
+            nc.scalar.copy(out=feats_row[:, tiles_of(c), 2 * HID:3 * HID], in_=relpos_ps[c])
 
         def transpose_words(c):
             words_ps[c] = psum_words.tile([P, CHUNK, 2, P], F32, name="words_ps", tag="words")

@@ -50,6 +50,8 @@ def tile_edgefeaturenet_pa_kernel(
         psum_words = ctx.enter_context(tc.psum_pool(name="psum_words", bufs=2))
         psum_acc = ctx.enter_context(tc.psum_pool(name="psum_acc", bufs=4))
 
+        node_pos = const.tile([P, POS_COLS], BF16)
+        nc.gpsimd.memset(node_pos[:], 0.0)
         ident_bf = const.tile([P, P], BF16)
         make_identity(nc, ident_bf[:])
         bin_index = const.tile([P, BINS + 1], F32)
@@ -60,8 +62,6 @@ def tile_edgefeaturenet_pa_kernel(
         ident_f32 = const.tile([P, P], F32)
         make_identity(nc, ident_f32[:])
 
-        node_pos = const.tile([P, POS_COLS], BF16)
-        nc.vector.memset(node_pos[:], 0.0)
         node_flow = const.tile([P, FLOW_COLS], BF16)
         nc.vector.memset(node_flow[:], 0.0)
         others_n2e = const.tile([P, TILES, HID], BF16)
@@ -202,10 +202,10 @@ def tile_edgefeaturenet_pa_kernel(
                 in1=above[:, tiles_of(c), :, 1:BINS + 1],
                 op=ALU.subtract,
             )
-            nc.gpsimd.tensor_scalar(
-                out=feats_row[:, tiles_of(c), FEATS - 2:FEATS], in0=flags[:, tiles_of(c), :],
-                scalar1=1.0, scalar2=0.0, op0=ALU.mult, op1=ALU.add,
-            )
+            if c == 0:
+                nc.gpsimd.tensor_scalar(
+                    out=feats_row[:, :, FEATS - 2:FEATS], in0=flags[:], scalar1=1.0, scalar2=0.0, op0=ALU.mult, op1=ALU.add
+                )
 
         def middle_matmuls(c):
             middle_ps[c] = psum_middle.tile([P, 2 * CHUNK * HID], F32, name="middle_ps")
@@ -245,15 +245,19 @@ def tile_edgefeaturenet_pa_kernel(
                 in_=grouped[c][:].rearrange("p l r j -> p (l r j)"),
             )
 
-        def quantise_w1(n):
-            w_grouped = work.tile([P, N_COLS, PACK], BF16, align_bytes=64)
+        w_grouped = {}
+
+        def regroup_w1(n):
+            w_grouped[n] = work.tile([P, N_COLS, PACK], BF16, name="w_grouped", align_bytes=64)
             nc.vector.tensor_copy(
-                out=w_grouped[:].rearrange("p (c i) j -> p c j i", i=4),
+                out=w_grouped[n][:].rearrange("p (c i) j -> p c j i", i=4),
                 in_=w_raw[:, :, n * N_COLS:(n + 1) * N_COLS].rearrange("p j (c i) -> p c j i", i=4),
             )
+
+        def quantise_w1(n):
             nc.vector.quantize_mx(
                 out=w_codes[:, n, :].bitcast(FP8X4), scales=w_scales[:, n, :],
-                in_=w_grouped[:].rearrange("p w j -> p (w j)"),
+                in_=w_grouped[n][:].rearrange("p w j -> p (w j)"),
             )
 
         def passes(c):
@@ -299,6 +303,8 @@ def tile_edgefeaturenet_pa_kernel(
 
         for s in range(-5, CHUNKS + 1):
             if s == -1:
+                for n in range(N_HALVES):
+                    regroup_w1(n)
                 for n in range(N_HALVES):
                     quantise_w1(n)
             if live(s + 1):

@@ -122,8 +122,10 @@ def tile_edgefeaturenet_pa_kernel(
             .to_broadcast([P, BATCH, NODES, HALF]),
             op=ALU.add,
         )
-        pos_ps = psum_words.tile([P, POS_COLS], F32, tag="words")
-        nc.tensor.matmul(out=pos_ps[:], lhsT=pick[:], rhs=node_pos[:], start=True, stop=True)
+        pos_ps = psum_words.tile([P, OWN_N2E], F32, tag="words")
+        nc.tensor.matmul(out=pos_ps[:], lhsT=pick[:], rhs=node_pos[:, 0:OWN_N2E], start=True, stop=True)
+        own_ps = psum_acc.tile([P, HID], BF16, tag="acc")
+        nc.tensor.matmul(out=own_ps[:], lhsT=pick[:], rhs=node_pos[:, OWN_N2E:POS_COLS], start=True, stop=True)
 
         own_pos = const.tile([P, OTH_TRANS], F32)
         nc.vector.tensor_copy(out=own_pos[:], in_=pos_ps[:, 0:OTH_TRANS])
@@ -148,8 +150,8 @@ def tile_edgefeaturenet_pa_kernel(
             op0=ALU.not_equal, op1=ALU.mult,
         )
 
-        own_n2e = const.tile([P, HID], BF16)
-        nc.scalar.copy(out=own_n2e[:], in_=pos_ps[:, OWN_N2E:POS_COLS])
+        feats_row = const.tile([P, TILES, FEATS], BF16)
+        nc.scalar.copy(out=feats_row[:, :, 0:HID], in_=own_ps[:].unsqueeze(1).to_broadcast([P, TILES, HID]))
 
         emb_t = const.tile([P, TILES, P], BF16)
         for half in range(2):
@@ -167,7 +169,6 @@ def tile_edgefeaturenet_pa_kernel(
         )
         nc.scalar.copy(out=flags[:, :, 1:2], in_=flow_ps[:, OTH_FLOW:FLOW_COLS].unsqueeze(2))
 
-        feats_row = const.tile([P, TILES, FEATS], BF16)
         row_words = feats_row[:].bitcast(F32)
         above = const.tile([P, TILES, 2, BINS + 1], BF16)
         w_codes = const.tile([P, N_HALVES, N_COLS], U32, align_bytes=64)
@@ -192,10 +193,6 @@ def tile_edgefeaturenet_pa_kernel(
             )
 
         def outer_features(c):
-            nc.gpsimd.tensor_scalar(
-                out=feats_row[:, tiles_of(c), 0:HID], in0=own_n2e[:].unsqueeze(1).to_broadcast([P, CHUNK, HID]),
-                scalar1=1.0, scalar2=0.0, op0=ALU.mult, op1=ALU.add,
-            )
             nc.gpsimd.tensor_tensor(
                 out=feats_row[:, tiles_of(c), 3 * HID:3 * HID + 2 * BINS].rearrange("p t (s k) -> p t s k", s=2),
                 in0=above[:, tiles_of(c), :, 0:BINS],

@@ -163,11 +163,11 @@ def tile_edgefeaturenet_pa_kernel(
 
         flow_ps = psum_words.tile([P, FLOW_COLS], F32, tag="words")
         nc.tensor.matmul(out=flow_ps[:], lhsT=pick[:], rhs=node_flow[:], start=True, stop=True)
-        flags = const.tile([P, TILES, 2], BF16)
         nc.scalar.copy(
-            out=flags[:, :, 0:1], in_=flow_ps[:, OWN_FLOW:OWN_FLOW + 1].unsqueeze(1).to_broadcast([P, TILES, 1])
+            out=feats_row[:, :, FEATS - 2:FEATS - 1],
+            in_=flow_ps[:, OWN_FLOW:OWN_FLOW + 1].unsqueeze(1).to_broadcast([P, TILES, 1]),
         )
-        nc.scalar.copy(out=flags[:, :, 1:2], in_=flow_ps[:, OTH_FLOW:FLOW_COLS].unsqueeze(2))
+        nc.scalar.copy(out=feats_row[:, :, FEATS - 1:FEATS], in_=flow_ps[:, OTH_FLOW:FLOW_COLS].unsqueeze(2))
 
         row_words = feats_row[:].bitcast(F32)
         above = const.tile([P, TILES, 2, BINS + 1], BF16)
@@ -192,17 +192,14 @@ def tile_edgefeaturenet_pa_kernel(
                 op=ALU.is_gt,
             )
 
-        def outer_features(c):
-            nc.gpsimd.tensor_tensor(
-                out=feats_row[:, tiles_of(c), 3 * HID:3 * HID + 2 * BINS].rearrange("p t (s k) -> p t s k", s=2),
-                in0=above[:, tiles_of(c), :, 0:BINS],
-                in1=above[:, tiles_of(c), :, 1:BINS + 1],
+        def bins(engine, first, count):
+            tiles = slice(first * CHUNK, (first + count) * CHUNK)
+            engine.tensor_tensor(
+                out=feats_row[:, tiles, 3 * HID:3 * HID + 2 * BINS].rearrange("p t (s k) -> p t s k", s=2),
+                in0=above[:, tiles, :, 0:BINS],
+                in1=above[:, tiles, :, 1:BINS + 1],
                 op=ALU.subtract,
             )
-            if c == 0:
-                nc.gpsimd.tensor_scalar(
-                    out=feats_row[:, :, FEATS - 2:FEATS], in0=flags[:], scalar1=1.0, scalar2=0.0, op0=ALU.mult, op1=ALU.add
-                )
 
         def middle_matmuls(c):
             middle_ps[c] = psum_middle.tile([P, 2 * CHUNK * HID], F32, name="middle_ps")
@@ -308,10 +305,15 @@ def tile_edgefeaturenet_pa_kernel(
                 quantise_features(s + 1)
             if live(s):
                 add_bias(s)
-            if live(s + 5) and (s + 5) % COMPARED == 0:
+            if s == -5:
+                compare(0)
+                compare(COMPARED)
+                bins(nc.vector, 0, COMPARED)
+                bins(nc.vector, COMPARED, COMPARED)
+            if s + 5 >= 2 * COMPARED and live(s + 5) and (s + 5) % COMPARED == 0:
                 compare(s + 5)
-            if live(s + 4):
-                outer_features(s + 4)
+            if s + 4 >= 2 * COMPARED and live(s + 4):
+                bins(nc.gpsimd, s + 4, 1)
             if live(s + 3):
                 transpose_words(s + 3)
             if live(s + 5):

@@ -26,7 +26,7 @@ CHUNKS = TILES // CHUNK
 COMPARED = 2
 N_COLS = 512
 N_HALVES = WIDTH // N_COLS
-SHARED_RELUS = (0, 2, 3)
+SHARED_RELUS = (1, 3)
 
 OWN_TRANS, OWN_SC, OTH_TRANS = 0, 16, 32
 OTH_SC = OTH_TRANS + TILES * XYZ
@@ -303,6 +303,8 @@ def tile_edgefeaturenet_pa_kernel(
                     quantise_w1(n)
             if live(s + 1):
                 quantise_features(s + 1)
+            if s + 4 >= 2 * COMPARED and live(s + 4) and (s + 4) % COMPARED == 0:
+                compare(s + 4)
             if live(s):
                 add_bias(s)
             if s == -5:
@@ -310,8 +312,6 @@ def tile_edgefeaturenet_pa_kernel(
                 compare(COMPARED)
                 bins(nc.vector, 0, COMPARED)
                 bins(nc.vector, COMPARED, COMPARED)
-            if s + 5 >= 2 * COMPARED and live(s + 5) and (s + 5) % COMPARED == 0:
-                compare(s + 5)
             if s + 4 >= 2 * COMPARED and live(s + 4):
                 bins(nc.gpsimd, s + 4, 1)
             if live(s + 3):

@@ -6,6 +6,7 @@ from concourse.masks import make_identity
 F32 = mybir.dt.float32
 BF16 = mybir.dt.bfloat16
 U32 = mybir.dt.uint32
+I32 = mybir.dt.int32
 U8 = mybir.dt.uint8
 FP8X4 = mybir.dt.float8_e4m3fn_x4
 ALU = mybir.AluOpType
@@ -23,15 +24,16 @@ TILES = PAIRS // P
 HALF = NODES // TILES
 CHUNK = 2
 CHUNKS = TILES // CHUNK
-COMPARED = 2
+HEAD_TILES = 4
+TURNED = 4
 N_COLS = 512
+PIECES = 4
 N_HALVES = WIDTH // N_COLS
-SHARED_RELUS = (1, 3)
+SHARED_RELUS = (1, 3, 5)
 
 OWN_TRANS, OWN_SC, OTH_TRANS = 0, 16, 32
 OTH_SC = OTH_TRANS + TILES * XYZ
-OWN_N2E = OTH_SC + TILES * XYZ
-POS_COLS = OWN_N2E + HID
+POS_COLS = OTH_SC + TILES * XYZ
 OWN_FLOW, OTH_FLOW, FLOW_COLS = 0, 16, 32
 
 FLOPS = 2 * PAIRS * FEATS * WIDTH + 2 * PAIRS * HID * HID
@@ -44,8 +46,8 @@ def tile_edgefeaturenet_pa_kernel(
     with ExitStack() as ctx:
         ctx.enter_context(tc.manual_schedule())
         const = ctx.enter_context(tc.tile_pool(name="const", bufs=1))
-        work = ctx.enter_context(tc.tile_pool(name="work", bufs=3))
-        stage = ctx.enter_context(tc.tile_pool(name="stage", bufs=6))
+        work = ctx.enter_context(tc.tile_pool(name="work", bufs=4))
+        stage = ctx.enter_context(tc.tile_pool(name="stage", bufs=TILES))
         psum_middle = ctx.enter_context(tc.psum_pool(name="psum_middle", bufs=2))
         psum_words = ctx.enter_context(tc.psum_pool(name="psum_words", bufs=2))
         psum_acc = ctx.enter_context(tc.psum_pool(name="psum_acc", bufs=4))
@@ -54,46 +56,64 @@ def tile_edgefeaturenet_pa_kernel(
         nc.gpsimd.memset(node_pos[:], 0.0)
         ident_bf = const.tile([P, P], BF16)
         make_identity(nc, ident_bf[:])
-        bin_index = const.tile([P, BINS + 1], F32)
+        bin_no = const.tile([P, 2, BINS - 1], BF16)
         nc.gpsimd.iota(
-            bin_index[:], pattern=[[1, BINS + 1]], base=0, channel_multiplier=0,
+            bin_no[:], pattern=[[1, 2], [1, BINS - 1]], base=1, channel_multiplier=0,
+            allow_small_or_imprecise_dtypes=True,
+        )
+        mid_no = const.tile([P, 2], BF16)
+        nc.gpsimd.iota(
+            mid_no[:], pattern=[[1 - BINS, 2]], base=BINS, channel_multiplier=0,
             allow_small_or_imprecise_dtypes=True,
         )
         ident_f32 = const.tile([P, P], F32)
         make_identity(nc, ident_f32[:])
 
-        node_flow = const.tile([P, FLOW_COLS], BF16)
-        nc.vector.memset(node_flow[:], 0.0)
-        others_n2e = const.tile([P, TILES, HID], BF16)
-        nc.vector.memset(others_n2e[:], 0.0)
-        bias_row = const.tile([P, HID], BF16)
-        nc.vector.memset(bias_row[:], 0.0)
         ones = const.tile([P, P], BF16)
         nc.vector.memset(ones[:], 1.0)
-
+        others_n2e = const.tile([P, HEAD_TILES, HID], BF16)
+        nc.vector.memset(others_n2e[:].bitcast(F32), 0.0)
+        bias_row = const.tile([P, HID], BF16)
+        nc.vector.memset(bias_row[:], 0.0)
+        node_flow = const.tile([P, FLOW_COLS], BF16)
+        nc.vector.memset(node_flow[:], 0.0)
+        node_n2e = const.tile([P, HID], BF16)
+        nc.vector.memset(node_n2e[64:P, :], 0.0)
         with nc.allow_non_contiguous_dma(reason="three values for each node"):
-            nc.sync.dma_start(out=node_pos[0:64, OWN_TRANS:OWN_TRANS + XYZ], in_=trans.rearrange("b n c -> (b n) c"))
-            nc.sync.dma_start(out=node_pos[0:64, OWN_SC:OWN_SC + XYZ], in_=sc_trans.rearrange("b n c -> (b n) c"))
+            nc.sync.dma_start(
+                out=node_pos[0:64, OWN_TRANS:OWN_TRANS + XYZ], in_=trans.rearrange("b n c -> (b n) c")
+            )
+            nc.sync.dma_start(
+                out=node_pos[0:64, OWN_SC:OWN_SC + XYZ], in_=sc_trans.rearrange("b n c -> (b n) c")
+            )
         nc.sync.dma_start(
             out=node_pos[64:68, OTH_TRANS:OTH_SC], in_=trans.rearrange("b (h t) c -> (b h) (t c)", h=HALF)
         )
         nc.sync.dma_start(
-            out=node_pos[64:68, OTH_SC:OWN_N2E], in_=sc_trans.rearrange("b (h t) c -> (b h) (t c)", h=HALF)
+            out=node_pos[64:68, OTH_SC:POS_COLS], in_=sc_trans.rearrange("b (h t) c -> (b h) (t c)", h=HALF)
         )
-        nc.sync.dma_start(out=node_pos[0:64, OWN_N2E:POS_COLS], in_=n2e.rearrange("b n f -> (b n) f"))
-        emb = const.tile([P, TILES, HID], BF16)
-        nc.sync.dma_start(
-            out=emb[:], in_=relpos_emb.rearrange("b i j h -> (b i j) h").rearrange("(p t) h -> p t h", t=TILES)
-        )
-        w_raw = const.tile([P, PACK, WIDTH], BF16)
-        w1_rows = W1.rearrange("(p j) w -> p j w", j=PACK)
-        for n in range(N_HALVES):
-            cols = slice(n * N_COLS, (n + 1) * N_COLS)
-            nc.sync.dma_start(out=w_raw[:, :, cols], in_=w1_rows[:, :, cols])
+        nc.sync.dma_start(out=node_n2e[0:64, :], in_=n2e.rearrange("b n f -> (b n) f"))
         w_rp = const.tile([P, HID], BF16)
         nc.sync.dma_start(out=w_rp[:], in_=W_rp)
-        nc.sync.dma_start(out=others_n2e[64:68, :, :], in_=n2e.rearrange("b (h t) f -> (b h) t f", h=HALF))
+        w1_rows = W1.rearrange("(p j) w -> p j w", j=PACK)
+        w_raw = {}
+
+        def load_w1(n):
+            w_raw[n] = const.tile([P, PACK, N_COLS], BF16, name="w_raw%d" % n)
+            nc.sync.dma_start(out=w_raw[n][:], in_=w1_rows[:, :, n * N_COLS:(n + 1) * N_COLS])
+
+        emb_rows = relpos_emb.rearrange("b i j h -> (b i j) h").rearrange("(p t) h -> p t h", t=TILES)
+        emb_head = const.tile([P, HEAD_TILES, HID], BF16)
+        nc.sync.dma_start(out=emb_head[:], in_=emb_rows[:, 0:HEAD_TILES, :])
+        load_w1(0)
+        nc.sync.dma_start(
+            out=others_n2e[64:68, :, :],
+            in_=n2e.rearrange("b (h t) f -> (b h) t f", h=HALF)[:, 0:HEAD_TILES, :],
+        )
         nc.sync.dma_start(out=bias_row[0:1, :], in_=b_rp.rearrange("(o f) -> o f", o=1))
+        emb_late = const.tile([P, TILES - HEAD_TILES, HID], BF16)
+        nc.sync.dma_start(out=emb_late[:], in_=emb_rows[:, HEAD_TILES:TILES, :])
+        load_w1(1)
         with nc.allow_non_contiguous_dma(reason="one value for each node"):
             nc.sync.dma_start(
                 out=node_flow[0:64, OWN_FLOW:OWN_FLOW + 1], in_=flow_mask.rearrange("b (n o) -> (b n) o", o=1)
@@ -103,15 +123,24 @@ def tile_edgefeaturenet_pa_kernel(
         )
         bias_all = const.tile([P, WIDTH], BF16)
         nc.sync.dma_start(out=bias_all[:], in_=b1.partition_broadcast(P))
+        late = TILES - HEAD_TILES
+        head_rows = const.tile([P, HEAD_TILES, FEATS], BF16)
+        late_rows = const.tile([P, late, FEATS], BF16)
+        for h in range(HALF):
+            nc.sync.dma_start(
+                out=late_rows[h:P:HALF, :, 0:HID],
+                in_=n2e.rearrange("b n f -> (b n) f").unsqueeze(1).to_broadcast([BATCH * NODES, late, HID]),
+            )
+        for b in range(BATCH):
+            for h in range(HALF):
+                first = h * TILES + HEAD_TILES
+                nc.sync.dma_start(
+                    out=late_rows[b * P // BATCH + h:(b + 1) * P // BATCH:HALF, :, HID:2 * HID],
+                    in_=n2e[b, first:first + late, :].unsqueeze(0).to_broadcast([NODES, late, HID]),
+                )
 
-        edge = const.tile([P, BINS + 1], F32)
-        nc.vector.tensor_scalar(
-            out=edge[:], in0=bin_index[:], scalar1=BIN_STEP, scalar2=MIN_BIN, op0=ALU.mult, op1=ALU.add
-        )
-        edge_sq = const.tile([P, BINS + 1], F32)
-        nc.vector.tensor_tensor(out=edge_sq[:], in0=edge[:], in1=edge[:], op=ALU.mult)
-        nc.vector.memset(edge_sq[:, BINS - 1:BINS], MAX_BIN * MAX_BIN)
-        nc.vector.memset(edge_sq[:, BINS:BINS + 1], FAR * FAR)
+        root = const.tile([P, 1], F32)
+        nc.scalar.activation(out=root[:], in_=ones[:, 0:1], func=ACT.Sqrt)
 
         pick = const.tile([P, P], BF16)
         nc.vector.tensor_tensor(
@@ -122,84 +151,96 @@ def tile_edgefeaturenet_pa_kernel(
             .to_broadcast([P, BATCH, NODES, HALF]),
             op=ALU.add,
         )
-        pos_ps = psum_words.tile([P, OWN_N2E], F32, tag="words")
-        nc.tensor.matmul(out=pos_ps[:], lhsT=pick[:], rhs=node_pos[:, 0:OWN_N2E], start=True, stop=True)
-        own_ps = psum_acc.tile([P, HID], BF16, tag="acc")
-        nc.tensor.matmul(out=own_ps[:], lhsT=pick[:], rhs=node_pos[:, OWN_N2E:POS_COLS], start=True, stop=True)
-
-        own_pos = const.tile([P, OTH_TRANS], F32)
-        nc.vector.tensor_copy(out=own_pos[:], in_=pos_ps[:, 0:OTH_TRANS])
-        delta = const.tile([P, 2, TILES, XYZ], F32)
-        nc.vector.tensor_tensor(
-            out=delta[:],
-            in0=pos_ps[:, OTH_TRANS:OWN_N2E].rearrange("p (s t c) -> p s t c", s=2, t=TILES),
-            in1=own_pos[:].rearrange("p (s x) -> p s x", s=2)[:, :, 0:XYZ].unsqueeze(2)
+        minus_pick = const.tile([P, P], BF16)
+        nc.vector.tensor_scalar_mul(out=minus_pick[:], in0=pick[:], scalar1=-1.0)
+        delta_ps = psum_words.tile([P, 2, TILES, XYZ], F32, tag="words")
+        nc.tensor.matmul(
+            out=delta_ps[:], lhsT=pick[:],
+            rhs=node_pos[:, OTH_TRANS:POS_COLS].rearrange("k (s t c) -> k s t c", s=2, t=TILES),
+            start=True, stop=False,
+        )
+        nc.tensor.matmul(
+            out=delta_ps[:], lhsT=minus_pick[:],
+            rhs=node_pos[:, 0:OTH_TRANS].rearrange("k (s x) -> k s x", s=2)[:, :, 0:XYZ].unsqueeze(2)
             .to_broadcast([P, 2, TILES, XYZ]),
-            op=ALU.subtract,
+            start=False, stop=True,
         )
         delta_sq = const.tile([P, 2, TILES, XYZ], F32)
-        nc.vector.tensor_tensor(out=delta_sq[:], in0=delta[:], in1=delta[:], op=ALU.mult)
+        nc.scalar.activation(out=delta_sq[:], in_=delta_ps[:], func=ACT.Square)
         raw_sq = const.tile([P, TILES, 2], F32)
         nc.vector.tensor_reduce(
             out=raw_sq[:].rearrange("p t s -> p s t"), in_=delta_sq[:], axis=mybir.AxisListType.X, op=ALU.add
         )
         dist_sq = const.tile([P, TILES, 2], F32)
         nc.vector.scalar_tensor_tensor(
-            out=dist_sq[:].rearrange("p t s -> p (t s)"), in0=raw_sq[:].rearrange("p t s -> p (t s)"),
-            scalar=MAX_BIN * MAX_BIN, in1=raw_sq[:].rearrange("p t s -> p (t s)"),
-            op0=ALU.not_equal, op1=ALU.mult,
+            out=dist_sq[:], in0=raw_sq[:], scalar=MAX_BIN * MAX_BIN, in1=raw_sq[:], op0=ALU.not_equal, op1=ALU.mult
         )
-
-        feats_row = const.tile([P, TILES, FEATS], BF16)
-        nc.scalar.copy(out=feats_row[:, :, 0:HID], in_=own_ps[:].unsqueeze(1).to_broadcast([P, TILES, HID]))
-
         emb_t = const.tile([P, TILES, P], BF16)
-        for half in range(2):
-            tiles = slice(half * TILES // 2, (half + 1) * TILES // 2)
-            emb_t_ps = psum_acc.tile([P, TILES // 2, P], BF16, tag="acc")
-            for l in range(TILES // 2):
-                nc.tensor.transpose(out=emb_t_ps[:, l, :], in_=emb[:, half * TILES // 2 + l, :], identity=ident_bf[:])
-            nc.scalar.copy(out=emb_t[:, tiles, :], in_=emb_t_ps[:])
 
-        flow_ps = psum_words.tile([P, FLOW_COLS], F32, tag="words")
-        nc.tensor.matmul(out=flow_ps[:], lhsT=pick[:], rhs=node_flow[:], start=True, stop=True)
-        nc.scalar.copy(
-            out=feats_row[:, :, FEATS - 2:FEATS - 1],
-            in_=flow_ps[:, OWN_FLOW:OWN_FLOW + 1].unsqueeze(1).to_broadcast([P, TILES, 1]),
-        )
-        nc.scalar.copy(out=feats_row[:, :, FEATS - 1:FEATS], in_=flow_ps[:, OTH_FLOW:FLOW_COLS].unsqueeze(2))
 
-        row_words = feats_row[:].bitcast(F32)
-        above = const.tile([P, TILES, 2, BINS + 1], BF16)
+        def rows(first, count):
+            if first < HEAD_TILES:
+                return head_rows[:, first:first + count, :]
+            return late_rows[:, first - HEAD_TILES:first - HEAD_TILES + count, :]
+
         w_codes = const.tile([P, N_HALVES, N_COLS], U32, align_bytes=64)
         w_scales = const.tile([P, N_HALVES, N_COLS], U8, align_bytes=64)
         f_codes = const.tile([P, CHUNKS, CHUNK * P], U32, align_bytes=64)
         f_scales = const.tile([P, CHUNKS, CHUNK * P], U8, align_bytes=64)
         out_rows = out.rearrange("b i j e -> (b i j) e").rearrange("(p t) e -> p t e", t=TILES)
         middle_ps, words_ps, grouped, acc, result = {}, {}, {}, {}, {}
+        emb_t_ps = {}
         relpos_ps, others_ps = {}, {}
 
         def tiles_of(c):
             return slice(c * CHUNK, (c + 1) * CHUNK)
 
-        def compare(c):
-            tiles = slice(c * CHUNK, (c + COMPARED) * CHUNK)
-            shape = [P, COMPARED * CHUNK * 2, BINS + 1]
-            nc.vector.tensor_tensor(
-                out=above[:, tiles, :, :].rearrange("p t s k -> p (t s) k"),
-                in0=dist_sq[:, tiles, :].rearrange("p t s -> p (t s)").unsqueeze(2).to_broadcast(shape),
-                in1=edge_sq[:].unsqueeze(1).to_broadcast(shape),
-                op=ALU.is_gt,
+        def emb_tile(t):
+            return emb_head[:, t, :] if t < HEAD_TILES else emb_late[:, t - HEAD_TILES, :]
+
+        def turn_emb(q):
+            emb_t_ps[q] = psum_acc.tile([P, TURNED, P], BF16, name="emb_t_ps", tag="acc")
+            for l in range(TURNED):
+                nc.tensor.transpose(out=emb_t_ps[q][:, l, :], in_=emb_tile(q * TURNED + l), identity=ident_bf[:])
+
+        def copy_emb(q):
+            nc.scalar.copy(out=emb_t[:, q * TURNED:(q + 1) * TURNED, :], in_=emb_t_ps[q][:])
+
+        def own_features():
+            nc.scalar.copy(
+                out=rows(0, HEAD_TILES)[:, :, 0:HID],
+                in_=own_row[:].unsqueeze(1).to_broadcast([P, HEAD_TILES, HID]),
             )
 
-        def bins(engine, first, count):
-            tiles = slice(first * CHUNK, (first + count) * CHUNK)
-            engine.tensor_tensor(
-                out=feats_row[:, tiles, 3 * HID:3 * HID + 2 * BINS].rearrange("p t (s k) -> p t s k", s=2),
-                in0=above[:, tiles, :, 0:BINS],
-                in1=above[:, tiles, :, 1:BINS + 1],
-                op=ALU.subtract,
+        def flow_features(first, count):
+            nc.scalar.copy(
+                out=rows(first, count)[:, :, FEATS - 2:FEATS - 1],
+                in_=flow_row[:, OWN_FLOW:OWN_FLOW + 1].unsqueeze(1).to_broadcast([P, count, 1]),
             )
+            nc.scalar.copy(
+                out=rows(first, count)[:, :, FEATS - 1:FEATS],
+                in_=flow_row[:, OTH_FLOW + first:OTH_FLOW + first + count].unsqueeze(2),
+            )
+
+        def middle_bins(first, count):
+            nc.vector.tensor_tensor(
+                out=rows(first, count)[:, :, 3 * HID + BINS - 1:3 * HID + BINS + 1],
+                in0=bin_of[:, first:first + count, :, 0],
+                in1=mid_no[:].unsqueeze(1).to_broadcast([P, count, 2]),
+                op=ALU.is_equal,
+            )
+
+        def bins(first, count):
+            shape = [P, count, (BINS - 1) // 2, 2]
+            for sc in range(2):
+                start = 3 * HID + sc * (BINS + 1)
+                nc.vector.tensor_tensor(
+                    out=rows(first, count)[:, :, start:start + BINS - 1]
+                    .rearrange("p t (m e) -> p t m e", e=2),
+                    in0=bin_of[:, first:first + count, sc, :].unsqueeze(2).to_broadcast(shape),
+                    in1=bin_no[:, sc, :].rearrange("p (m e) -> p m e", e=2).unsqueeze(1).to_broadcast(shape),
+                    op=ALU.is_equal,
+                )
 
         def middle_matmuls(c):
             middle_ps[c] = psum_middle.tile([P, 2 * CHUNK * HID], F32, name="middle_ps")
@@ -210,21 +251,26 @@ def tile_edgefeaturenet_pa_kernel(
             )
             for l in range(CHUNK):
                 t = c * CHUNK + l
-                nc.tensor.matmul(out=others_ps[c][:, l, :], lhsT=pick[:], rhs=others_n2e[:, t, :], start=True, stop=True)
+                if t < HEAD_TILES:
+                    nc.tensor.matmul(
+                        out=others_ps[c][:, l, :], lhsT=pick[:], rhs=others_n2e[:, t, :], start=True, stop=True
+                    )
                 nc.tensor.matmul(out=relpos_ps[c][:, l, :], lhsT=emb_t[:, t, :], rhs=w_rp[:], start=True, stop=False)
                 nc.tensor.matmul(out=relpos_ps[c][:, l, :], lhsT=ones[:], rhs=bias_row[:], start=False, stop=True)
 
         def middle_features(c):
-            nc.scalar.copy(out=feats_row[:, tiles_of(c), HID:2 * HID], in_=others_ps[c])
-            nc.scalar.copy(out=feats_row[:, tiles_of(c), 2 * HID:3 * HID], in_=relpos_ps[c])
+            if c * CHUNK < HEAD_TILES:
+                nc.scalar.copy(out=rows(c * CHUNK, CHUNK)[:, :, HID:2 * HID], in_=others_ps[c])
+            nc.scalar.copy(out=rows(c * CHUNK, CHUNK)[:, :, 2 * HID:3 * HID], in_=relpos_ps[c])
 
         def transpose_words(c):
             words_ps[c] = psum_words.tile([P, CHUNK, 2, P], F32, name="words_ps", tag="words")
+            words = rows(c * CHUNK, CHUNK).bitcast(F32)
             for l in range(CHUNK):
                 for u in range(2):
                     nc.tensor.transpose(
                         out=words_ps[c][:, l, u, :],
-                        in_=row_words[:, c * CHUNK + l, u:FEATS // 2:2],
+                        in_=words[:, l, u:FEATS // 2:2],
                         identity=ident_f32[:],
                     )
 
@@ -241,11 +287,15 @@ def tile_edgefeaturenet_pa_kernel(
 
         w_grouped = {}
 
-        def regroup_w1(n):
-            w_grouped[n] = work.tile([P, N_COLS, PACK], BF16, name="w_grouped", align_bytes=64)
+        def regroup_w1(piece):
+            n, part = divmod(piece, PIECES)
+            if part == 0:
+                w_grouped[n] = work.tile([P, N_COLS, PACK], BF16, name="w_grouped", align_bytes=64)
+            width = N_COLS // PIECES
+            cols = slice(part * width, (part + 1) * width)
             nc.vector.tensor_copy(
-                out=w_grouped[n][:].rearrange("p (c i) j -> p c j i", i=4),
-                in_=w_raw[:, :, n * N_COLS:(n + 1) * N_COLS].rearrange("p j (c i) -> p c j i", i=4),
+                out=w_grouped[n][:, cols, :].rearrange("p (c i) j -> p c j i", i=4),
+                in_=w_raw[n][:, :, cols].rearrange("p j (c i) -> p c j i", i=4),
             )
 
         def quantise_w1(n):
@@ -268,14 +318,13 @@ def tile_edgefeaturenet_pa_kernel(
                         stop=True,
                     )
 
-        def add_bias(c):
-            for l in range(CHUNK):
-                result[c, l] = stage.tile([P, WIDTH], F32, name="result")
-                for n in range(N_HALVES):
-                    cols = slice(n * N_COLS, (n + 1) * N_COLS)
-                    nc.vector.tensor_tensor(
-                        out=result[c, l][:, cols], in0=acc[c, l, n][:], in1=bias_all[:, cols], op=ALU.add
-                    )
+        def add_bias(c, l):
+            result[c, l] = stage.tile([P, WIDTH], F32, name="result")
+            for n in range(N_HALVES):
+                cols = slice(n * N_COLS, (n + 1) * N_COLS)
+                nc.vector.tensor_tensor(
+                    out=result[c, l][:, cols], in0=acc[c, l, n][:], in1=bias_all[:, cols], op=ALU.add
+                )
 
         def relu_and_store(c, l):
             if l == 0 and c in SHARED_RELUS:
@@ -295,36 +344,94 @@ def tile_edgefeaturenet_pa_kernel(
         def live(c):
             return 0 <= c < CHUNKS
 
-        for s in range(-5, CHUNKS + 1):
-            if s == -1:
-                for n in range(N_HALVES):
-                    regroup_w1(n)
-                for n in range(N_HALVES):
-                    quantise_w1(n)
+        own_ps = psum_acc.tile([P, HID], BF16, tag="acc")
+        nc.tensor.matmul(out=own_ps[:], lhsT=pick[:], rhs=node_n2e[:], start=True, stop=True)
+        own_row = const.tile([P, HID], BF16)
+        nc.scalar.copy(out=own_row[:], in_=own_ps[:])
+        own_features()
+        dist = const.tile([P, TILES, 2], F32)
+        nc.scalar.activation(out=dist[:], in_=dist_sq[:], func=ACT.Sqrt)
+        turn_emb(0)
+        copy_emb(0)
+        middle_matmuls(0)
+        middle_features(0)
+        middle_matmuls(1)
+        middle_features(1)
+        flow_ps = psum_words.tile([P, FLOW_COLS], F32, tag="words")
+        nc.tensor.matmul(out=flow_ps[:], lhsT=pick[:], rhs=node_flow[:], start=True, stop=True)
+        flow_row = const.tile([P, FLOW_COLS], BF16)
+        nc.scalar.copy(out=flow_row[:], in_=flow_ps[:])
+        flow_features(0, HEAD_TILES)
+        turn_emb(1)
+        copy_emb(1)
+        edge_no = const.tile([P, TILES, 2], I32)
+        nc.vector.tensor_scalar(
+            out=edge_no[:], in0=dist[:], scalar1=MAX_BIN, scalar2=1.0 / BIN_STEP, op0=ALU.min, op1=ALU.mult
+        )
+        regroup_w1(0)
+        edge = const.tile([P, TILES, 2], F32)
+        nc.vector.tensor_scalar(
+            out=edge[:], in0=edge_no[:], scalar1=BIN_STEP, scalar2=MIN_BIN, op0=ALU.mult, op1=ALU.add
+        )
+        regroup_w1(1)
+        edge_sq = const.tile([P, TILES, 2], F32)
+        nc.vector.tensor_tensor(out=edge_sq[:], in0=edge[:], in1=edge[:], op=ALU.mult)
+        regroup_w1(2)
+        beyond = const.tile([P, TILES, 2], F32)
+        nc.vector.tensor_tensor(out=beyond[:], in0=dist_sq[:], in1=edge_sq[:], op=ALU.is_gt)
+        regroup_w1(3)
+        beyond_far = const.tile([P, TILES, 2], F32)
+        nc.vector.scalar_tensor_tensor(
+            out=beyond_far[:], in0=dist_sq[:], scalar=FAR * FAR, in1=beyond[:], op0=ALU.is_ge, op1=ALU.add
+        )
+        bin_of = const.tile([P, TILES, 2, 2], BF16)
+        nc.vector.tensor_tensor(
+            out=bin_of[:].rearrange("p t s e -> p (t s) e"),
+            in0=edge_no[:].rearrange("p t s -> p (t s)").unsqueeze(2).to_broadcast([P, 2 * TILES, 2]),
+            in1=beyond_far[:].rearrange("p t s -> p (t s)").unsqueeze(2).to_broadcast([P, 2 * TILES, 2]),
+            op=ALU.add,
+        )
+        middle_bins(0, HEAD_TILES)
+        bins(0, HEAD_TILES)
+        transpose_words(0)
+        transpose_words(1)
+        middle_matmuls(2)
+        turn_emb(2)
+        turn_emb(3)
+        group_words(0)
+        middle_matmuls(3)
+        for piece in range(PIECES, N_HALVES * PIECES):
+            regroup_w1(piece)
+        group_words(1)
+        copy_emb(2)
+        copy_emb(3)
+        flow_features(HEAD_TILES, late)
+        middle_features(2)
+        quantise_w1(0)
+        quantise_w1(1)
+        quantise_features(0)
+        passes(0)
+        middle_bins(HEAD_TILES, late)
+        bins(HEAD_TILES, late)
+        middle_features(3)
+        for s in range(CHUNKS + 1):
+            if live(s):
+                add_bias(s, 0)
             if live(s + 1):
                 quantise_features(s + 1)
-            if s + 4 >= 2 * COMPARED and live(s + 4) and (s + 4) % COMPARED == 0:
-                compare(s + 4)
             if live(s):
-                add_bias(s)
-            if s == -5:
-                compare(0)
-                compare(COMPARED)
-                bins(nc.vector, 0, COMPARED)
-                bins(nc.vector, COMPARED, COMPARED)
-            if s + 4 >= 2 * COMPARED and live(s + 4):
-                bins(nc.gpsimd, s + 4, 1)
-            if live(s + 3):
-                transpose_words(s + 3)
-            if live(s + 5):
-                middle_matmuls(s + 5)
+                add_bias(s, 1)
+            if live(s + 2):
+                transpose_words(s + 2)
             if live(s + 1):
                 passes(s + 1)
+            if live(s + 4):
+                middle_matmuls(s + 4)
             if live(s - 1):
                 relu_and_store(s - 1, 1)
             if live(s + 2):
                 group_words(s + 2)
-            if live(s + 4):
-                middle_features(s + 4)
             if live(s):
                 relu_and_store(s, 0)
+            if live(s + 4):
+                middle_features(s + 4)

@@ -71,7 +71,7 @@ def tile_edgefeaturenet_pa_kernel(
 
         ones = const.tile([P, P], BF16)
         nc.vector.memset(ones[:], 1.0)
-        others_n2e = const.tile([P, HEAD_TILES, HID], BF16)
+        others_n2e = const.tile([P, TILES, HID], BF16)
         nc.vector.memset(others_n2e[:].bitcast(F32), 0.0)
         bias_row = const.tile([P, HID], BF16)
         nc.vector.memset(bias_row[:], 0.0)
@@ -107,8 +107,7 @@ def tile_edgefeaturenet_pa_kernel(
         nc.sync.dma_start(out=emb_head[:], in_=emb_rows[:, 0:HEAD_TILES, :])
         load_w1(0)
         nc.sync.dma_start(
-            out=others_n2e[64:68, :, :],
-            in_=n2e.rearrange("b (h t) f -> (b h) t f", h=HALF)[:, 0:HEAD_TILES, :],
+            out=others_n2e[64:68, :, :], in_=n2e.rearrange("b (h t) f -> (b h) t f", h=HALF),
         )
         nc.sync.dma_start(out=bias_row[0:1, :], in_=b_rp.rearrange("(o f) -> o f", o=1))
         emb_late = const.tile([P, TILES - HEAD_TILES, HID], BF16)
@@ -126,19 +125,6 @@ def tile_edgefeaturenet_pa_kernel(
         late = TILES - HEAD_TILES
         head_rows = const.tile([P, HEAD_TILES, FEATS], BF16)
         late_rows = const.tile([P, late, FEATS], BF16)
-        for h in range(HALF):
-            nc.sync.dma_start(
-                out=late_rows[h:P:HALF, :, 0:HID],
-                in_=n2e.rearrange("b n f -> (b n) f").unsqueeze(1).to_broadcast([BATCH * NODES, late, HID]),
-            )
-        for b in range(BATCH):
-            for h in range(HALF):
-                first = h * TILES + HEAD_TILES
-                nc.sync.dma_start(
-                    out=late_rows[b * P // BATCH + h:(b + 1) * P // BATCH:HALF, :, HID:2 * HID],
-                    in_=n2e[b, first:first + late, :].unsqueeze(0).to_broadcast([NODES, late, HID]),
-                )
-
         root = const.tile([P, 1], F32)
         nc.scalar.activation(out=root[:], in_=ones[:, 0:1], func=ACT.Sqrt)
 
@@ -251,16 +237,12 @@ def tile_edgefeaturenet_pa_kernel(
             )
             for l in range(CHUNK):
                 t = c * CHUNK + l
-                if t < HEAD_TILES:
-                    nc.tensor.matmul(
-                        out=others_ps[c][:, l, :], lhsT=pick[:], rhs=others_n2e[:, t, :], start=True, stop=True
-                    )
+                nc.tensor.matmul(out=others_ps[c][:, l, :], lhsT=pick[:], rhs=others_n2e[:, t, :], start=True, stop=True)
                 nc.tensor.matmul(out=relpos_ps[c][:, l, :], lhsT=emb_t[:, t, :], rhs=w_rp[:], start=True, stop=False)
                 nc.tensor.matmul(out=relpos_ps[c][:, l, :], lhsT=ones[:], rhs=bias_row[:], start=False, stop=True)
 
         def middle_features(c):
-            if c * CHUNK < HEAD_TILES:
-                nc.scalar.copy(out=rows(c * CHUNK, CHUNK)[:, :, HID:2 * HID], in_=others_ps[c])
+            nc.scalar.copy(out=rows(c * CHUNK, CHUNK)[:, :, HID:2 * HID], in_=others_ps[c])
             nc.scalar.copy(out=rows(c * CHUNK, CHUNK)[:, :, 2 * HID:3 * HID], in_=relpos_ps[c])
 
         def transpose_words(c):
@@ -349,6 +331,9 @@ def tile_edgefeaturenet_pa_kernel(
         own_row = const.tile([P, HID], BF16)
         nc.scalar.copy(out=own_row[:], in_=own_ps[:])
         own_features()
+        nc.sync.dma_start(
+            out=late_rows[:, :, 0:HID], in_=own_row[:].unsqueeze(1).to_broadcast([P, TILES - HEAD_TILES, HID])
+        )
         dist = const.tile([P, TILES, 2], F32)
         nc.scalar.activation(out=dist[:], in_=dist_sq[:], func=ACT.Sqrt)
         turn_emb(0)
@@ -429,9 +414,9 @@ def tile_edgefeaturenet_pa_kernel(
                 middle_matmuls(s + 4)
             if live(s - 1):
                 relu_and_store(s - 1, 1)
+            if live(s + 3) and s > 0:
+                middle_features(s + 3)
             if live(s + 2):
                 group_words(s + 2)
             if live(s):
                 relu_and_store(s, 0)
-            if live(s + 4):
-                middle_features(s + 4)

@@ -29,12 +29,13 @@ TURNED = 4
 N_COLS = 512
 PIECES = 4
 N_HALVES = WIDTH // N_COLS
-SHARED_RELUS = (1, 3, 5)
 
 OWN_TRANS, OWN_SC, OTH_TRANS = 0, 16, 32
 OTH_SC = OTH_TRANS + TILES * XYZ
 POS_COLS = OTH_SC + TILES * XYZ
 OWN_FLOW, OTH_FLOW, FLOW_COLS = 0, 16, 32
+
+VCOLS = {(c, 0): N_COLS for c in (1, 2, 3, 4)}
 
 FLOPS = 2 * PAIRS * FEATS * WIDTH + 2 * PAIRS * HID * HID
 
@@ -92,9 +93,6 @@ def tile_edgefeaturenet_pa_kernel(
         nc.sync.dma_start(
             out=node_pos[64:68, OTH_SC:POS_COLS], in_=sc_trans.rearrange("b (h t) c -> (b h) (t c)", h=HALF)
         )
-        nc.sync.dma_start(out=node_n2e[0:64, :], in_=n2e.rearrange("b n f -> (b n) f"))
-        w_rp = const.tile([P, HID], BF16)
-        nc.sync.dma_start(out=w_rp[:], in_=W_rp)
         w1_rows = W1.rearrange("(p j) w -> p j w", j=PACK)
         w_raw = {}
 
@@ -102,16 +100,17 @@ def tile_edgefeaturenet_pa_kernel(
             w_raw[n] = const.tile([P, PACK, N_COLS], BF16, name="w_raw%d" % n)
             nc.sync.dma_start(out=w_raw[n][:], in_=w1_rows[:, :, n * N_COLS:(n + 1) * N_COLS])
 
+        load_w1(0)
+        nc.sync.dma_start(out=node_n2e[0:64, :], in_=n2e.rearrange("b n f -> (b n) f"))
         emb_rows = relpos_emb.rearrange("b i j h -> (b i j) h").rearrange("(p t) h -> p t h", t=TILES)
         emb_head = const.tile([P, HEAD_TILES, HID], BF16)
         nc.sync.dma_start(out=emb_head[:], in_=emb_rows[:, 0:HEAD_TILES, :])
-        load_w1(0)
+        w_rp = const.tile([P, HID], BF16)
+        nc.sync.dma_start(out=w_rp[:], in_=W_rp)
         nc.sync.dma_start(
             out=others_n2e[64:68, :, :], in_=n2e.rearrange("b (h t) f -> (b h) t f", h=HALF),
         )
         nc.sync.dma_start(out=bias_row[0:1, :], in_=b_rp.rearrange("(o f) -> o f", o=1))
-        emb_late = const.tile([P, TILES - HEAD_TILES, HID], BF16)
-        nc.sync.dma_start(out=emb_late[:], in_=emb_rows[:, HEAD_TILES:TILES, :])
         load_w1(1)
         with nc.allow_non_contiguous_dma(reason="one value for each node"):
             nc.sync.dma_start(
@@ -120,6 +119,8 @@ def tile_edgefeaturenet_pa_kernel(
         nc.sync.dma_start(
             out=node_flow[64:68, OTH_FLOW:FLOW_COLS], in_=flow_mask.rearrange("b (h t) -> (b h) t", h=HALF)
         )
+        emb_late = const.tile([P, TILES - HEAD_TILES, HID], BF16)
+        nc.sync.dma_start(out=emb_late[:], in_=emb_rows[:, HEAD_TILES:TILES, :])
         bias_all = const.tile([P, WIDTH], BF16)
         nc.sync.dma_start(out=bias_all[:], in_=b1.partition_broadcast(P))
         late = TILES - HEAD_TILES
@@ -176,7 +177,6 @@ def tile_edgefeaturenet_pa_kernel(
         out_rows = out.rearrange("b i j e -> (b i j) e").rearrange("(p t) e -> p t e", t=TILES)
         middle_ps, words_ps, grouped, acc, result = {}, {}, {}, {}, {}
         emb_t_ps = {}
-        relpos_ps, others_ps = {}, {}
 
         def tiles_of(c):
             return slice(c * CHUNK, (c + 1) * CHUNK)
@@ -229,21 +229,20 @@ def tile_edgefeaturenet_pa_kernel(
                 )
 
         def middle_matmuls(c):
-            middle_ps[c] = psum_middle.tile([P, 2 * CHUNK * HID], F32, name="middle_ps")
-            relpos_ps[c] = middle_ps[c][:, 0:CHUNK * HID].rearrange("p (l f) -> p l f", l=CHUNK)
-            others_ps[c] = (
-                middle_ps[c][:, CHUNK * HID:CHUNK * HID + CHUNK * HID // 2].bitcast(BF16)
-                .rearrange("p (l f) -> p l f", l=CHUNK)
-            )
+            middle_ps[c] = psum_middle.tile([P, CHUNK, 2 * HID], BF16, name="middle_ps")
             for l in range(CHUNK):
                 t = c * CHUNK + l
-                nc.tensor.matmul(out=others_ps[c][:, l, :], lhsT=pick[:], rhs=others_n2e[:, t, :], start=True, stop=True)
-                nc.tensor.matmul(out=relpos_ps[c][:, l, :], lhsT=emb_t[:, t, :], rhs=w_rp[:], start=True, stop=False)
-                nc.tensor.matmul(out=relpos_ps[c][:, l, :], lhsT=ones[:], rhs=bias_row[:], start=False, stop=True)
+                others, projected = middle_ps[c][:, l, 0:HID], middle_ps[c][:, l, HID:2 * HID]
+                nc.tensor.matmul(out=others, lhsT=pick[:], rhs=others_n2e[:, t, :], start=True, stop=True)
+                nc.tensor.matmul(out=projected, lhsT=ones[:], rhs=bias_row[:], start=True, stop=False)
+                nc.tensor.matmul(out=projected, lhsT=emb_t[:, t, :], rhs=w_rp[:], start=False, stop=True)
 
         def middle_features(c):
-            nc.scalar.copy(out=rows(c * CHUNK, CHUNK)[:, :, HID:2 * HID], in_=others_ps[c])
-            nc.scalar.copy(out=rows(c * CHUNK, CHUNK)[:, :, 2 * HID:3 * HID], in_=relpos_ps[c])
+            for first in (0, HID):
+                nc.scalar.copy(
+                    out=rows(c * CHUNK, CHUNK)[:, :, HID + first:2 * HID + first],
+                    in_=middle_ps[c][:, :, first:first + HID],
+                )
 
         def transpose_words(c):
             words_ps[c] = psum_words.tile([P, CHUNK, 2, P], F32, name="words_ps", tag="words")
@@ -308,24 +307,36 @@ def tile_edgefeaturenet_pa_kernel(
                     out=result[c, l][:, cols], in0=acc[c, l, n][:], in1=bias_all[:, cols], op=ALU.add
                 )
 
-        def relu_and_store(c, l):
-            if l == 0 and c in SHARED_RELUS:
-                nc.scalar.activation(out=result[c, l][:, 0:N_COLS], in_=result[c, l][:, 0:N_COLS], func=ACT.Relu)
+        def vector_columns(c, l):
+            return VCOLS.get((c, l), WIDTH)
+
+        def vector_relu(c, l):
+            first = vector_columns(c, l)
+            if first < WIDTH:
                 nc.vector.tensor_scalar_max(
-                    out=result[c, l][:, N_COLS:WIDTH], in0=result[c, l][:, N_COLS:WIDTH], scalar1=0.0
+                    out=result[c, l][:, first:WIDTH], in0=result[c, l][:, first:WIDTH], scalar1=0.0
                 )
-                nc.sync.dma_start(out=out_rows[:, c * CHUNK + l, :], in_=result[c, l][:])
-                return
+
+        def relu_and_store(c, l):
             last = c == CHUNKS - 1 and l == CHUNK - 1
             width = N_COLS if last else WIDTH
             for first in range(0, WIDTH, width):
-                cols = slice(first, first + width)
-                nc.scalar.activation(out=result[c, l][:, cols], in_=result[c, l][:, cols], func=ACT.Relu)
-                nc.sync.dma_start(out=out_rows[:, c * CHUNK + l, cols], in_=result[c, l][:, cols])
+                end = min(first + width, vector_columns(c, l))
+                if end > first:
+                    nc.scalar.activation(
+                        out=result[c, l][:, first:end], in_=result[c, l][:, first:end], func=ACT.Relu
+                    )
+                nc.sync.dma_start(
+                    out=out_rows[:, c * CHUNK + l, first:first + width], in_=result[c, l][:, first:first + width]
+                )
 
         def live(c):
             return 0 <= c < CHUNKS
 
+        dist = const.tile([P, TILES, 2], F32)
+        nc.scalar.activation(out=dist[:], in_=dist_sq[:], func=ACT.Sqrt)
+        turn_emb(0)
+        copy_emb(0)
         own_ps = psum_acc.tile([P, HID], BF16, tag="acc")
         nc.tensor.matmul(out=own_ps[:], lhsT=pick[:], rhs=node_n2e[:], start=True, stop=True)
         own_row = const.tile([P, HID], BF16)
@@ -334,41 +345,39 @@ def tile_edgefeaturenet_pa_kernel(
         nc.sync.dma_start(
             out=late_rows[:, :, 0:HID], in_=own_row[:].unsqueeze(1).to_broadcast([P, TILES - HEAD_TILES, HID])
         )
-        dist = const.tile([P, TILES, 2], F32)
-        nc.scalar.activation(out=dist[:], in_=dist_sq[:], func=ACT.Sqrt)
-        turn_emb(0)
-        copy_emb(0)
         middle_matmuls(0)
         middle_features(0)
-        middle_matmuls(1)
-        middle_features(1)
         flow_ps = psum_words.tile([P, FLOW_COLS], F32, tag="words")
         nc.tensor.matmul(out=flow_ps[:], lhsT=pick[:], rhs=node_flow[:], start=True, stop=True)
         flow_row = const.tile([P, FLOW_COLS], BF16)
         nc.scalar.copy(out=flow_row[:], in_=flow_ps[:])
         flow_features(0, HEAD_TILES)
+        middle_matmuls(1)
+        middle_features(1)
         turn_emb(1)
         copy_emb(1)
+        regroup_w1(0)
         edge_no = const.tile([P, TILES, 2], I32)
         nc.vector.tensor_scalar(
             out=edge_no[:], in0=dist[:], scalar1=MAX_BIN, scalar2=1.0 / BIN_STEP, op0=ALU.min, op1=ALU.mult
         )
-        regroup_w1(0)
+        regroup_w1(1)
         edge = const.tile([P, TILES, 2], F32)
         nc.vector.tensor_scalar(
             out=edge[:], in0=edge_no[:], scalar1=BIN_STEP, scalar2=MIN_BIN, op0=ALU.mult, op1=ALU.add
         )
-        regroup_w1(1)
+        regroup_w1(2)
         edge_sq = const.tile([P, TILES, 2], F32)
         nc.vector.tensor_tensor(out=edge_sq[:], in0=edge[:], in1=edge[:], op=ALU.mult)
-        regroup_w1(2)
+        regroup_w1(3)
         beyond = const.tile([P, TILES, 2], F32)
         nc.vector.tensor_tensor(out=beyond[:], in0=dist_sq[:], in1=edge_sq[:], op=ALU.is_gt)
-        regroup_w1(3)
+        regroup_w1(4)
         beyond_far = const.tile([P, TILES, 2], F32)
         nc.vector.scalar_tensor_tensor(
             out=beyond_far[:], in0=dist_sq[:], scalar=FAR * FAR, in1=beyond[:], op0=ALU.is_ge, op1=ALU.add
         )
+        regroup_w1(5)
         bin_of = const.tile([P, TILES, 2, 2], BF16)
         nc.vector.tensor_tensor(
             out=bin_of[:].rearrange("p t s e -> p (t s) e"),
@@ -385,7 +394,7 @@ def tile_edgefeaturenet_pa_kernel(
         turn_emb(3)
         group_words(0)
         middle_matmuls(3)
-        for piece in range(PIECES, N_HALVES * PIECES):
+        for piece in range(6, N_HALVES * PIECES):
             regroup_w1(piece)
         group_words(1)
         copy_emb(2)
@@ -402,9 +411,12 @@ def tile_edgefeaturenet_pa_kernel(
         for s in range(CHUNKS + 1):
             if live(s):
                 add_bias(s, 0)
+            if live(s - 1):
+                vector_relu(s - 1, 1)
             if live(s + 1):
                 quantise_features(s + 1)
             if live(s):
+                vector_relu(s, 0)
                 add_bias(s, 1)
             if live(s + 2):
                 transpose_words(s + 2)

@@ -35,7 +35,8 @@ OTH_SC = OTH_TRANS + TILES * XYZ
 POS_COLS = OTH_SC + TILES * XYZ
 OWN_FLOW, OTH_FLOW, FLOW_COLS = 0, 16, 32
 
-VCOLS = {(c, 0): N_COLS for c in (1, 2, 3, 4)}
+GTILES = tuple((c, 0, 1) for c in range(CHUNKS - 2))
+VCOLS = {}
 
 FLOPS = 2 * PAIRS * FEATS * WIDTH + 2 * PAIRS * HID * HID
 
@@ -303,16 +304,34 @@ def tile_edgefeaturenet_pa_kernel(
             result[c, l] = stage.tile([P, WIDTH], F32, name="result")
             for n in range(N_HALVES):
                 cols = slice(n * N_COLS, (n + 1) * N_COLS)
-                nc.vector.tensor_tensor(
-                    out=result[c, l][:, cols], in0=acc[c, l, n][:], in1=bias_all[:, cols], op=ALU.add
-                )
+                if (c, l, n) in GTILES:
+                    nc.vector.scalar_tensor_tensor(
+                        out=result[c, l][:, cols], in0=bias_all[:, cols], scalar=-1.0, in1=acc[c, l, n][:],
+                        op0=ALU.mult, op1=ALU.max,
+                    )
+                else:
+                    nc.vector.tensor_tensor(
+                        out=result[c, l][:, cols], in0=acc[c, l, n][:], in1=bias_all[:, cols], op=ALU.add
+                    )
+
+        def finish_on_gpsimd(c, l):
+            for n in range(N_HALVES):
+                cols = slice(n * N_COLS, (n + 1) * N_COLS)
+                if (c, l, n) in GTILES:
+                    nc.gpsimd.tensor_tensor(
+                        out=result[c, l][:, cols], in0=result[c, l][:, cols], in1=bias_all[:, cols], op=ALU.add
+                    )
 
         def vector_columns(c, l):
+            if (c, l, 0) in GTILES:
+                return 0
+            if (c, l, 1) in GTILES:
+                return N_COLS
             return VCOLS.get((c, l), WIDTH)
 
         def vector_relu(c, l):
             first = vector_columns(c, l)
-            if first < WIDTH:
+            if first < WIDTH and (c, l, 1) not in GTILES:
                 nc.vector.tensor_scalar_max(
                     out=result[c, l][:, first:WIDTH], in0=result[c, l][:, first:WIDTH], scalar1=0.0
                 )
@@ -412,10 +431,12 @@ def tile_edgefeaturenet_pa_kernel(
             if live(s):
                 add_bias(s, 0)
             if live(s - 1):
+                finish_on_gpsimd(s - 1, 1)
                 vector_relu(s - 1, 1)
             if live(s + 1):
                 quantise_features(s + 1)
             if live(s):
+                finish_on_gpsimd(s, 0)
                 vector_relu(s, 0)
                 add_bias(s, 1)
             if live(s + 2):

@@ -24,6 +24,7 @@ TILES = PAIRS // P
 HALF = NODES // TILES
 CHUNK = 2
 CHUNKS = TILES // CHUNK
+QUARTER = P // 4
 HEAD_TILES = 4
 TURNED = 4
 N_COLS = 512
@@ -123,7 +124,7 @@ def tile_edgefeaturenet_pa_kernel(
         emb_late = const.tile([P, TILES - HEAD_TILES, HID], BF16)
         nc.sync.dma_start(out=emb_late[:], in_=emb_rows[:, HEAD_TILES:TILES, :])
         bias_all = const.tile([P, WIDTH], BF16)
-        nc.sync.dma_start(out=bias_all[:], in_=b1.partition_broadcast(P))
+        nc.sync.dma_start(out=bias_all[0:QUARTER, :], in_=b1.partition_broadcast(QUARTER))
         late = TILES - HEAD_TILES
         head_rows = const.tile([P, HEAD_TILES, FEATS], BF16)
         late_rows = const.tile([P, late, FEATS], BF16)
@@ -364,6 +365,8 @@ def tile_edgefeaturenet_pa_kernel(
         nc.sync.dma_start(
             out=late_rows[:, :, 0:HID], in_=own_row[:].unsqueeze(1).to_broadcast([P, TILES - HEAD_TILES, HID])
         )
+        for first in range(QUARTER, P, QUARTER):
+            nc.sync.dma_start(out=bias_all[first:first + QUARTER, :], in_=bias_all[0:QUARTER, :])
         middle_matmuls(0)
         middle_features(0)
         flow_ps = psum_words.tile([P, FLOW_COLS], F32, tag="words")

from contextlib import ExitStack

import concourse.mybir as mybir
from concourse.masks import make_identity

F32 = mybir.dt.float32
BF16 = mybir.dt.bfloat16
U32 = mybir.dt.uint32
I32 = mybir.dt.int32
U8 = mybir.dt.uint8
FP8X4 = mybir.dt.float8_e4m3fn_x4
ALU = mybir.AluOpType
ACT = mybir.ActivationFunctionType

BATCH, NODES, XYZ, HID, BINS, WIDTH = 2, 32, 3, 128, 63, 1024
FEATS = 3 * HID + 2 * BINS + 2
MIN_BIN, MAX_BIN, FAR = 0.001, 20.0, 1e8
BIN_STEP = (MAX_BIN - MIN_BIN) / (BINS - 1)

P = 128
PACK = 4
PAIRS = BATCH * NODES * NODES
TILES = PAIRS // P
HALF = NODES // TILES
CHUNK = 2
CHUNKS = TILES // CHUNK
QUARTER = P // 4
HEAD_TILES = 4
TURNED = 4
N_COLS = 512
PIECES = 4
N_HALVES = WIDTH // N_COLS

OWN_TRANS, OWN_SC, OTH_TRANS = 0, 16, 32
OTH_SC = OTH_TRANS + TILES * XYZ
POS_COLS = OTH_SC + TILES * XYZ
OWN_FLOW, OTH_FLOW, FLOW_COLS = 0, 16, 32

GTILES = tuple((c, 0, 1) for c in range(CHUNKS - 2))
VCOLS = {}

FLOPS = 2 * PAIRS * FEATS * WIDTH + 2 * PAIRS * HID * HID


def tile_edgefeaturenet_pa_kernel(
    tc, n2e, relpos_emb, trans, sc_trans, flow_mask, W_rp, b_rp, W1, b1, out
):
    nc = tc.nc
    with ExitStack() as ctx:
        ctx.enter_context(tc.manual_schedule())
        const = ctx.enter_context(tc.tile_pool(name="const", bufs=1))
        work = ctx.enter_context(tc.tile_pool(name="work", bufs=4))
        stage = ctx.enter_context(tc.tile_pool(name="stage", bufs=TILES))
        psum_middle = ctx.enter_context(tc.psum_pool(name="psum_middle", bufs=2))
        psum_words = ctx.enter_context(tc.psum_pool(name="psum_words", bufs=2))
        psum_acc = ctx.enter_context(tc.psum_pool(name="psum_acc", bufs=4))

        node_pos = const.tile([P, POS_COLS], BF16)
        nc.gpsimd.memset(node_pos[:], 0.0)
        ident_bf = const.tile([P, P], BF16)
        make_identity(nc, ident_bf[:])
        bin_no = const.tile([P, 2, BINS - 1], BF16)
        nc.gpsimd.iota(
            bin_no[:], pattern=[[1, 2], [1, BINS - 1]], base=1, channel_multiplier=0,
            allow_small_or_imprecise_dtypes=True,
        )
        mid_no = const.tile([P, 2], BF16)
        nc.gpsimd.iota(
            mid_no[:], pattern=[[1 - BINS, 2]], base=BINS, channel_multiplier=0,
            allow_small_or_imprecise_dtypes=True,
        )
        ident_f32 = const.tile([P, P], F32)
        make_identity(nc, ident_f32[:])

        ones = const.tile([P, P], BF16)
        nc.vector.memset(ones[:], 1.0)
        others_n2e = const.tile([P, TILES, HID], BF16)
        nc.vector.memset(others_n2e[:].bitcast(F32), 0.0)
        bias_row = const.tile([P, HID], BF16)
        nc.vector.memset(bias_row[:], 0.0)
        node_flow = const.tile([P, FLOW_COLS], BF16)
        nc.vector.memset(node_flow[:], 0.0)
        node_n2e = const.tile([P, HID], BF16)
        nc.vector.memset(node_n2e[64:P, :], 0.0)
        with nc.allow_non_contiguous_dma(reason="three values for each node"):
            nc.sync.dma_start(
                out=node_pos[0:64, OWN_TRANS:OWN_TRANS + XYZ], in_=trans.rearrange("b n c -> (b n) c")
            )
            nc.sync.dma_start(
                out=node_pos[0:64, OWN_SC:OWN_SC + XYZ], in_=sc_trans.rearrange("b n c -> (b n) c")
            )
        nc.sync.dma_start(
            out=node_pos[64:68, OTH_TRANS:OTH_SC], in_=trans.rearrange("b (h t) c -> (b h) (t c)", h=HALF)
        )
        nc.sync.dma_start(
            out=node_pos[64:68, OTH_SC:POS_COLS], in_=sc_trans.rearrange("b (h t) c -> (b h) (t c)", h=HALF)
        )
        w1_rows = W1.rearrange("(p j) w -> p j w", j=PACK)
        w_raw = {}

        def load_w1(n):
            w_raw[n] = const.tile([P, PACK, N_COLS], BF16, name="w_raw%d" % n)
            nc.sync.dma_start(out=w_raw[n][:], in_=w1_rows[:, :, n * N_COLS:(n + 1) * N_COLS])

        load_w1(0)
        nc.sync.dma_start(out=node_n2e[0:64, :], in_=n2e.rearrange("b n f -> (b n) f"))
        emb_rows = relpos_emb.rearrange("b i j h -> (b i j) h").rearrange("(p t) h -> p t h", t=TILES)
        emb_head = const.tile([P, HEAD_TILES, HID], BF16)
        nc.sync.dma_start(out=emb_head[:], in_=emb_rows[:, 0:HEAD_TILES, :])
        w_rp = const.tile([P, HID], BF16)
        nc.sync.dma_start(out=w_rp[:], in_=W_rp)
        nc.sync.dma_start(
            out=others_n2e[64:68, :, :], in_=n2e.rearrange("b (h t) f -> (b h) t f", h=HALF),
        )
        nc.sync.dma_start(out=bias_row[0:1, :], in_=b_rp.rearrange("(o f) -> o f", o=1))
        load_w1(1)
        with nc.allow_non_contiguous_dma(reason="one value for each node"):
            nc.sync.dma_start(
                out=node_flow[0:64, OWN_FLOW:OWN_FLOW + 1], in_=flow_mask.rearrange("b (n o) -> (b n) o", o=1)
            )
        nc.sync.dma_start(
            out=node_flow[64:68, OTH_FLOW:FLOW_COLS], in_=flow_mask.rearrange("b (h t) -> (b h) t", h=HALF)
        )
        emb_late = const.tile([P, TILES - HEAD_TILES, HID], BF16)
        nc.sync.dma_start(out=emb_late[:], in_=emb_rows[:, HEAD_TILES:TILES, :])
        bias_all = const.tile([P, WIDTH], BF16)
        nc.sync.dma_start(out=bias_all[0:QUARTER, :], in_=b1.partition_broadcast(QUARTER))
        late = TILES - HEAD_TILES
        head_rows = const.tile([P, HEAD_TILES, FEATS], BF16)
        late_rows = const.tile([P, late, FEATS], BF16)
        root = const.tile([P, 1], F32)
        nc.scalar.activation(out=root[:], in_=ones[:, 0:1], func=ACT.Sqrt)

        pick = const.tile([P, P], BF16)
        nc.vector.tensor_tensor(
            out=pick[:].rearrange("k (b i h) -> k b i h", b=BATCH, h=HALF),
            in0=ident_bf[:, 0:64].rearrange("k (b i) -> k b i", b=BATCH).unsqueeze(3)
            .to_broadcast([P, BATCH, NODES, HALF]),
            in1=ident_bf[:, 64:68].rearrange("k (b h) -> k b h", b=BATCH).unsqueeze(2)
            .to_broadcast([P, BATCH, NODES, HALF]),
            op=ALU.add,
        )
        minus_pick = const.tile([P, P], BF16)
        nc.vector.tensor_scalar_mul(out=minus_pick[:], in0=pick[:], scalar1=-1.0)
        delta_ps = psum_words.tile([P, 2, TILES, XYZ], F32, tag="words")
        nc.tensor.matmul(
            out=delta_ps[:], lhsT=pick[:],
            rhs=node_pos[:, OTH_TRANS:POS_COLS].rearrange("k (s t c) -> k s t c", s=2, t=TILES),
            start=True, stop=False,
        )
        nc.tensor.matmul(
            out=delta_ps[:], lhsT=minus_pick[:],
            rhs=node_pos[:, 0:OTH_TRANS].rearrange("k (s x) -> k s x", s=2)[:, :, 0:XYZ].unsqueeze(2)
            .to_broadcast([P, 2, TILES, XYZ]),
            start=False, stop=True,
        )
        delta_sq = const.tile([P, 2, TILES, XYZ], F32)
        nc.scalar.activation(out=delta_sq[:], in_=delta_ps[:], func=ACT.Square)
        raw_sq = const.tile([P, TILES, 2], F32)
        nc.vector.tensor_reduce(
            out=raw_sq[:].rearrange("p t s -> p s t"), in_=delta_sq[:], axis=mybir.AxisListType.X, op=ALU.add
        )
        dist_sq = const.tile([P, TILES, 2], F32)
        nc.vector.scalar_tensor_tensor(
            out=dist_sq[:], in0=raw_sq[:], scalar=MAX_BIN * MAX_BIN, in1=raw_sq[:], op0=ALU.not_equal, op1=ALU.mult
        )
        emb_t = const.tile([P, TILES, P], BF16)


        def rows(first, count):
            if first < HEAD_TILES:
                return head_rows[:, first:first + count, :]
            return late_rows[:, first - HEAD_TILES:first - HEAD_TILES + count, :]

        w_codes = const.tile([P, N_HALVES, N_COLS], U32, align_bytes=64)
        w_scales = const.tile([P, N_HALVES, N_COLS], U8, align_bytes=64)
        f_codes = const.tile([P, CHUNKS, CHUNK * P], U32, align_bytes=64)
        f_scales = const.tile([P, CHUNKS, CHUNK * P], U8, align_bytes=64)
        out_rows = out.rearrange("b i j e -> (b i j) e").rearrange("(p t) e -> p t e", t=TILES)
        middle_ps, words_ps, grouped, acc, result = {}, {}, {}, {}, {}
        emb_t_ps = {}

        def tiles_of(c):
            return slice(c * CHUNK, (c + 1) * CHUNK)

        def emb_tile(t):
            return emb_head[:, t, :] if t < HEAD_TILES else emb_late[:, t - HEAD_TILES, :]

        def turn_emb(q):
            emb_t_ps[q] = psum_acc.tile([P, TURNED, P], BF16, name="emb_t_ps", tag="acc")
            for l in range(TURNED):
                nc.tensor.transpose(out=emb_t_ps[q][:, l, :], in_=emb_tile(q * TURNED + l), identity=ident_bf[:])

        def copy_emb(q):
            nc.scalar.copy(out=emb_t[:, q * TURNED:(q + 1) * TURNED, :], in_=emb_t_ps[q][:])

        def own_features():
            nc.scalar.copy(
                out=rows(0, HEAD_TILES)[:, :, 0:HID],
                in_=own_row[:].unsqueeze(1).to_broadcast([P, HEAD_TILES, HID]),
            )

        def flow_features(first, count):
            nc.scalar.copy(
                out=rows(first, count)[:, :, FEATS - 2:FEATS - 1],
                in_=flow_row[:, OWN_FLOW:OWN_FLOW + 1].unsqueeze(1).to_broadcast([P, count, 1]),
            )
            nc.scalar.copy(
                out=rows(first, count)[:, :, FEATS - 1:FEATS],
                in_=flow_row[:, OTH_FLOW + first:OTH_FLOW + first + count].unsqueeze(2),
            )

        def middle_bins(first, count):
            nc.vector.tensor_tensor(
                out=rows(first, count)[:, :, 3 * HID + BINS - 1:3 * HID + BINS + 1],
                in0=bin_of[:, first:first + count, :, 0],
                in1=mid_no[:].unsqueeze(1).to_broadcast([P, count, 2]),
                op=ALU.is_equal,
            )

        def bins(first, count):
            shape = [P, count, (BINS - 1) // 2, 2]
            for sc in range(2):
                start = 3 * HID + sc * (BINS + 1)
                nc.vector.tensor_tensor(
                    out=rows(first, count)[:, :, start:start + BINS - 1]
                    .rearrange("p t (m e) -> p t m e", e=2),
                    in0=bin_of[:, first:first + count, sc, :].unsqueeze(2).to_broadcast(shape),
                    in1=bin_no[:, sc, :].rearrange("p (m e) -> p m e", e=2).unsqueeze(1).to_broadcast(shape),
                    op=ALU.is_equal,
                )

        def middle_matmuls(c):
            middle_ps[c] = psum_middle.tile([P, CHUNK, 2 * HID], BF16, name="middle_ps")
            for l in range(CHUNK):
                t = c * CHUNK + l
                others, projected = middle_ps[c][:, l, 0:HID], middle_ps[c][:, l, HID:2 * HID]
                nc.tensor.matmul(out=others, lhsT=pick[:], rhs=others_n2e[:, t, :], start=True, stop=True)
                nc.tensor.matmul(out=projected, lhsT=ones[:], rhs=bias_row[:], start=True, stop=False)
                nc.tensor.matmul(out=projected, lhsT=emb_t[:, t, :], rhs=w_rp[:], start=False, stop=True)

        def middle_features(c):
            for first in (0, HID):
                nc.scalar.copy(
                    out=rows(c * CHUNK, CHUNK)[:, :, HID + first:2 * HID + first],
                    in_=middle_ps[c][:, :, first:first + HID],
                )

        def transpose_words(c):
            words_ps[c] = psum_words.tile([P, CHUNK, 2, P], F32, name="words_ps", tag="words")
            words = rows(c * CHUNK, CHUNK).bitcast(F32)
            for l in range(CHUNK):
                for u in range(2):
                    nc.tensor.transpose(
                        out=words_ps[c][:, l, u, :],
                        in_=words[:, l, u:FEATS // 2:2],
                        identity=ident_f32[:],
                    )

        def group_words(c):
            grouped[c] = work.tile([P, CHUNK, P, PACK], BF16, name="grouped", align_bytes=64)
            nc.scalar.copy(out=grouped[c][:].bitcast(F32), in_=words_ps[c][:].rearrange("p l u r -> p l r u"))

        def quantise_features(c):
            nc.vector.quantize_mx(
                out=f_codes[:, c, :].bitcast(FP8X4),
                scales=f_scales[:, c, :],
                in_=grouped[c][:].rearrange("p l r j -> p (l r j)"),
            )

        w_grouped = {}

        def regroup_w1(piece):
            n, part = divmod(piece, PIECES)
            if part == 0:
                w_grouped[n] = work.tile([P, N_COLS, PACK], BF16, name="w_grouped", align_bytes=64)
            width = N_COLS // PIECES
            cols = slice(part * width, (part + 1) * width)
            nc.vector.tensor_copy(
                out=w_grouped[n][:, cols, :].rearrange("p (c i) j -> p c j i", i=4),
                in_=w_raw[n][:, :, cols].rearrange("p j (c i) -> p c j i", i=4),
            )

        def quantise_w1(n):
            nc.vector.quantize_mx(
                out=w_codes[:, n, :].bitcast(FP8X4), scales=w_scales[:, n, :],
                in_=w_grouped[n][:].rearrange("p w j -> p (w j)"),
            )

        def passes(c):
            for l in range(CHUNK):
                for n in range(N_HALVES):
                    acc[c, l, n] = psum_acc.tile([P, N_COLS], F32, name="acc", tag="acc")
                    nc.tensor.matmul_mx(
                        out=acc[c, l, n][:],
                        lhsT=f_codes[:, c, l * P:(l + 1) * P].bitcast(FP8X4),
                        lhsT_scale=f_scales[:, c, l * P:(l + 1) * P],
                        rhs=w_codes[:, n, :].bitcast(FP8X4),
                        rhs_scale=w_scales[:, n, :],
                        start=True,
                        stop=True,
                    )

        def add_bias(c, l):
            result[c, l] = stage.tile([P, WIDTH], F32, name="result")
            for n in range(N_HALVES):
                cols = slice(n * N_COLS, (n + 1) * N_COLS)
                if (c, l, n) in GTILES:
                    nc.vector.scalar_tensor_tensor(
                        out=result[c, l][:, cols], in0=bias_all[:, cols], scalar=-1.0, in1=acc[c, l, n][:],
                        op0=ALU.mult, op1=ALU.max,
                    )
                else:
                    nc.vector.tensor_tensor(
                        out=result[c, l][:, cols], in0=acc[c, l, n][:], in1=bias_all[:, cols], op=ALU.add
                    )

        def finish_on_gpsimd(c, l):
            for n in range(N_HALVES):
                cols = slice(n * N_COLS, (n + 1) * N_COLS)
                if (c, l, n) in GTILES:
                    nc.gpsimd.tensor_tensor(
                        out=result[c, l][:, cols], in0=result[c, l][:, cols], in1=bias_all[:, cols], op=ALU.add
                    )

        def vector_columns(c, l):
            if (c, l, 0) in GTILES:
                return 0
            if (c, l, 1) in GTILES:
                return N_COLS
            return VCOLS.get((c, l), WIDTH)

        def vector_relu(c, l):
            first = vector_columns(c, l)
            if first < WIDTH and (c, l, 1) not in GTILES:
                nc.vector.tensor_scalar_max(
                    out=result[c, l][:, first:WIDTH], in0=result[c, l][:, first:WIDTH], scalar1=0.0
                )

        def relu_and_store(c, l):
            last = c == CHUNKS - 1 and l == CHUNK - 1
            width = N_COLS if last else WIDTH
            for first in range(0, WIDTH, width):
                end = min(first + width, vector_columns(c, l))
                if end > first:
                    nc.scalar.activation(
                        out=result[c, l][:, first:end], in_=result[c, l][:, first:end], func=ACT.Relu
                    )
                nc.sync.dma_start(
                    out=out_rows[:, c * CHUNK + l, first:first + width], in_=result[c, l][:, first:first + width]
                )

        def live(c):
            return 0 <= c < CHUNKS

        dist = const.tile([P, TILES, 2], F32)
        nc.scalar.activation(out=dist[:], in_=dist_sq[:], func=ACT.Sqrt)
        turn_emb(0)
        copy_emb(0)
        own_ps = psum_acc.tile([P, HID], BF16, tag="acc")
        nc.tensor.matmul(out=own_ps[:], lhsT=pick[:], rhs=node_n2e[:], start=True, stop=True)
        own_row = const.tile([P, HID], BF16)
        nc.scalar.copy(out=own_row[:], in_=own_ps[:])
        own_features()
        nc.sync.dma_start(
            out=late_rows[:, :, 0:HID], in_=own_row[:].unsqueeze(1).to_broadcast([P, TILES - HEAD_TILES, HID])
        )
        for first in range(QUARTER, P, QUARTER):
            nc.sync.dma_start(out=bias_all[first:first + QUARTER, :], in_=bias_all[0:QUARTER, :])
        middle_matmuls(0)
        middle_features(0)
        flow_ps = psum_words.tile([P, FLOW_COLS], F32, tag="words")
        nc.tensor.matmul(out=flow_ps[:], lhsT=pick[:], rhs=node_flow[:], start=True, stop=True)
        flow_row = const.tile([P, FLOW_COLS], BF16)
        nc.scalar.copy(out=flow_row[:], in_=flow_ps[:])
        flow_features(0, HEAD_TILES)
        middle_matmuls(1)
        middle_features(1)
        turn_emb(1)
        copy_emb(1)
        regroup_w1(0)
        edge_no = const.tile([P, TILES, 2], I32)
        nc.vector.tensor_scalar(
            out=edge_no[:], in0=dist[:], scalar1=MAX_BIN, scalar2=1.0 / BIN_STEP, op0=ALU.min, op1=ALU.mult
        )
        regroup_w1(1)
        edge = const.tile([P, TILES, 2], F32)
        nc.vector.tensor_scalar(
            out=edge[:], in0=edge_no[:], scalar1=BIN_STEP, scalar2=MIN_BIN, op0=ALU.mult, op1=ALU.add
        )
        regroup_w1(2)
        edge_sq = const.tile([P, TILES, 2], F32)
        nc.vector.tensor_tensor(out=edge_sq[:], in0=edge[:], in1=edge[:], op=ALU.mult)
        regroup_w1(3)
        beyond = const.tile([P, TILES, 2], F32)
        nc.vector.tensor_tensor(out=beyond[:], in0=dist_sq[:], in1=edge_sq[:], op=ALU.is_gt)
        regroup_w1(4)
        beyond_far = const.tile([P, TILES, 2], F32)
        nc.vector.scalar_tensor_tensor(
            out=beyond_far[:], in0=dist_sq[:], scalar=FAR * FAR, in1=beyond[:], op0=ALU.is_ge, op1=ALU.add
        )
        regroup_w1(5)
        bin_of = const.tile([P, TILES, 2, 2], BF16)
        nc.vector.tensor_tensor(
            out=bin_of[:].rearrange("p t s e -> p (t s) e"),
            in0=edge_no[:].rearrange("p t s -> p (t s)").unsqueeze(2).to_broadcast([P, 2 * TILES, 2]),
            in1=beyond_far[:].rearrange("p t s -> p (t s)").unsqueeze(2).to_broadcast([P, 2 * TILES, 2]),
            op=ALU.add,
        )
        middle_bins(0, HEAD_TILES)
        bins(0, HEAD_TILES)
        transpose_words(0)
        transpose_words(1)
        middle_matmuls(2)
        turn_emb(2)
        turn_emb(3)
        group_words(0)
        middle_matmuls(3)
        for piece in range(6, N_HALVES * PIECES):
            regroup_w1(piece)
        group_words(1)
        copy_emb(2)
        copy_emb(3)
        flow_features(HEAD_TILES, late)
        middle_features(2)
        quantise_w1(0)
        quantise_w1(1)
        quantise_features(0)
        passes(0)
        middle_bins(HEAD_TILES, late)
        bins(HEAD_TILES, late)
        middle_features(3)
        for s in range(CHUNKS + 1):
            if live(s):
                add_bias(s, 0)
            if live(s - 1):
                finish_on_gpsimd(s - 1, 1)
                vector_relu(s - 1, 1)
            if live(s + 1):
                quantise_features(s + 1)
            if live(s):
                finish_on_gpsimd(s, 0)
                vector_relu(s, 0)
                add_bias(s, 1)
            if live(s + 2):
                transpose_words(s + 2)
            if live(s + 1):
                passes(s + 1)
            if live(s + 4):
                middle_matmuls(s + 4)
            if live(s - 1):
                relu_and_store(s - 1, 1)
            if live(s + 3) and s > 0:
                middle_features(s + 3)
            if live(s + 2):
                group_words(s + 2)
            if live(s):
                relu_and_store(s, 0)
